import numpy as np
import ml_dtypes


def mxq(x, axis, fmt="e4m3"):
    dtype, down = {"e4m3": (ml_dtypes.float8_e4m3fn, 7), "e5m2": (ml_dtypes.float8_e5m2, 14)}[fmt]
    v = np.moveaxis(np.asarray(x, np.float32).astype(ml_dtypes.bfloat16).astype(np.float64), axis, -1)
    blocks = v.reshape(v.shape[:-1] + (-1, 32))
    amax = np.abs(blocks).max(-1, keepdims=True)
    byte = np.maximum(np.where(amax > 0, np.frexp(amax)[1] - 1 + 127, 0) - down, 1)
    scale = np.exp2(byte - 127.0)
    codes = (blocks / scale).astype(np.float32).astype(dtype).astype(np.float64)
    return np.moveaxis((codes * scale).reshape(v.shape), -1, axis)


WIDE = False


def mx_kscale(k):
    if not WIDE:
        return np.ones(k)
    levels = np.array([10, -10, 5, -5, 0])
    if k % 512:
        return np.exp2(np.random.permutation(np.resize(levels, k // 32))).repeat(32)
    a = np.empty((k // 512, 16))
    for p in range(k // 512):
        a[p, :8] = np.random.permutation(np.resize(levels, 8))
        for g in range(8):
            far = levels[np.abs(levels - a[p, g]) >= 10]
            a[p, g + 8] = far[np.random.randint(len(far))]
    return np.exp2(a.ravel()).repeat(32)


BF16 = ml_dtypes.bfloat16


def bf(x):
    return np.asarray(x, np.float32).astype(BF16)


def f64(x):
    return np.asarray(x).astype(np.float64)


B, S, H, N_HEADS, N_KV, D, QB, ORIG_MAX_POS = 1, 1024, 2048, 16, 4, 128, 512, 8192
ROPE_BASE = 5.0e5
ROPE_FACTOR = 8.0
LOW_FREQ, HIGH_FREQ = 1.0, 4.0


def llama3_cos_sin():
    inv_freq = 1.0 / (ROPE_BASE ** (np.arange(0, D, 2) / D))
    wavelen = 2.0 * np.pi / inv_freq
    smooth = np.clip((ORIG_MAX_POS / wavelen - LOW_FREQ) / (HIGH_FREQ - LOW_FREQ), 0.0, 1.0)
    new_inv_freq = (1.0 - smooth) * (inv_freq / ROPE_FACTOR) + smooth * inv_freq
    freqs = np.arange(S)[:, None] * new_inv_freq[None, :]
    emb = np.concatenate([freqs, freqs], axis=-1)
    return np.cos(emb), np.sin(emb)


def rotate_half(x):
    x1, x2 = x[..., : D // 2], x[..., D // 2:]
    return np.concatenate([-x2, x1], axis=-1)


def apply_rope(x, cos, sin):
    return x * cos[None, None, :, :] + rotate_half(x) * sin[None, None, :, :]


def draw0():
    s = mx_kscale(H)
    return {"hidden_states": bf(np.random.standard_normal((B, S, H)) * s),
            "wq": bf(np.random.standard_normal((N_HEADS * D, H)) / np.sqrt(H) / s[None, :]),
            "wk": bf(np.random.standard_normal((N_KV * D, H)) / np.sqrt(H) / s[None, :])}


def core(hidden_states, wq, wk):
    xq = mxq(f64(hidden_states), 2, "e4m3")
    q = (xq @ mxq(f64(wq), 1, "e4m3").T).reshape(B, S, N_HEADS, D).transpose(0, 2, 1, 3)
    k = (xq @ mxq(f64(wk), 1, "e4m3").T).reshape(B, S, N_KV, D).transpose(0, 2, 1, 3)
    cos, sin = llama3_cos_sin()
    return apply_rope(q, cos, sin), apply_rope(k, cos, sin)


def e4m3fn_bytes(y):
    return np.clip(np.asarray(y, np.float64), -448.0, 448.0).astype(np.float32).astype(ml_dtypes.float8_e4m3fn).view(np.uint8)


def e4m3fn_values(b):
    return np.asarray(b, np.uint8).view(ml_dtypes.float8_e4m3fn).astype(np.float64)


def setup_inputs():
    d = draw0()
    x0 = np.asarray(d['wq']).astype(np.float64)
    s = (np.max(np.abs(x0), axis=(0,), keepdims=True) / 448.0).astype(np.float32)
    out = {}
    for k, v in d.items():
        if k == 'wq':
            out['wq_bytes'] = e4m3fn_bytes(x0 / s.astype(np.float64))
            out['wq_scale'] = s
        else:
            out[k] = v
    return out


def reference(hidden_states, wq_bytes, wq_scale, wk):
    return core(hidden_states, e4m3fn_values(wq_bytes) * wq_scale.astype(np.float64), wk)

@@ -1,0 +1,344 @@
+from contextlib import ExitStack
+
+import concourse.mybir as mybir
+from concourse.masks import make_identity
+
+S, H, D = 1024, 2048, 128
+Q_HEADS, KV_HEADS = 16, 4
+ROPE_BASE, ROPE_FACTOR = 5.0e5, 8.0
+LOW_FREQ, HIGH_FREQ, ORIG_MAX_POS = 1.0, 4.0, 8192
+
+FLOPS = 2 * S * H * (Q_HEADS + KV_HEADS) * D
+
+F32 = mybir.dt.float32
+BF16 = mybir.dt.bfloat16
+I32 = mybir.dt.int32
+U32 = mybir.dt.uint32
+U8 = mybir.dt.uint8
+FP8 = mybir.dt.float8_e4m3fn
+FP8X4 = mybir.dt.float8_e4m3fn_x4
+ALU = mybir.AluOpType
+ACT = mybir.ActivationFunctionType
+
+P = 128
+PASSES = H // (4 * P)
+TOKEN_TILES = S // P
+HALF = D // 2
+GROUP_HEADS = 4
+GROUPS = (Q_HEADS + KV_HEADS) // GROUP_HEADS
+N = GROUP_HEADS * D
+
+PI = 3.141592653589793
+TWO_PI = 2.0 * PI
+TWO_PI_HIGH = 6.28125
+TWO_PI_LOW = TWO_PI - TWO_PI_HIGH
+
+OFFLOAD = {0: (1, 3, 5), 1: (1, 5), 2: (1, 3, 5), 3: (1, 5), 4: ()}
+VECTOR_ADDS = ((4, 6),)
+
+
+def llama3_smooth(j):
+    wavelen = TWO_PI * ROPE_BASE ** (2.0 * j / D)
+    return min(max((ORIG_MAX_POS / wavelen - LOW_FREQ) / (HIGH_FREQ - LOW_FREQ), 0.0), 1.0)
+
+
+def llama3_frequency(j):
+    inv_freq = ROPE_BASE ** (-2.0 * j / D)
+    smooth = llama3_smooth(j)
+    return (1.0 - smooth) * inv_freq / ROPE_FACTOR + smooth * inv_freq
+
+
+def tile_stickyllamaattention_pa_kernel(tc, hidden_states, wq_bytes, wq_scale, wk, out_0, out_1):
+    nc = tc.nc
+
+    hidden_tiles = hidden_states.rearrange("o (p i) k -> i p (o k)", i=TOKEN_TILES)
+    wk_rows = wk.rearrange("(r p) k -> r p k", p=P)
+    wq_groups = wq_bytes.rearrange("(c r p) k -> c p r k", r=GROUP_HEADS, p=P)
+    q_view = out_0.rearrange("o h (p i) d -> p (o h) i d", i=TOKEN_TILES)
+    k_view = out_1.rearrange("o h (p i) d -> p (o h) i d", i=TOKEN_TILES)
+
+    with ExitStack() as ctx:
+        const = ctx.enter_context(tc.tile_pool(name="const", bufs=1))
+        raw = ctx.enter_context(tc.tile_pool(name="raw", bufs=1))
+        xpool = ctx.enter_context(tc.tile_pool(name="xpool", bufs=6))
+        widep = ctx.enter_context(tc.tile_pool(name="widep", bufs=4))
+        groupedp = ctx.enter_context(tc.tile_pool(name="groupedp", bufs=2))
+        codes = ctx.enter_context(tc.tile_pool(name="codes", bufs=1))
+        wcodes = ctx.enter_context(tc.tile_pool(name="wcodes", bufs=2))
+        ropep = ctx.enter_context(tc.tile_pool(name="ropep", bufs=3))
+        stagep = ctx.enter_context(tc.tile_pool(name="stagep", bufs=2))
+        psum_t = ctx.enter_context(tc.psum_pool(name="psum_t", bufs=4))
+        psum_a = ctx.enter_context(tc.psum_pool(name="psum_a", bufs=4))
+
+        warm = const.tile([P, 2], F32, name="warm")
+        nc.vector.memset(warm[:, 0:1], 0.0)
+        nc.scalar.activation(out=warm[:, 1:2], in_=warm[:, 0:1], func=ACT.Sin)
+
+        scale4 = const.tile([P, PASSES, 4], F32, name="scale4")
+        nc.scalar.dma_start(out=scale4[:], in_=wq_scale.rearrange("o (g p t) -> p (o g) t", p=P, t=4))
+        wq_raw = []
+        for c in range(GROUPS - 1):
+            wq_raw.append(raw.tile([P, GROUP_HEADS, H], U8, name="wq_raw%d" % c))
+        wk_raw = {}
+        for gp in range(2):
+            for r in range(GROUP_HEADS):
+                wk_raw[(gp, r)] = raw.tile([P, H // 2], BF16, name="wk_raw%d_%d" % (gp, r))
+        x_raw = {}
+
+        def load_hidden(i):
+            x_raw[i] = xpool.tile([P, H], BF16, name="x_raw")
+            nc.sync.dma_start(out=x_raw[i][:], in_=hidden_tiles[i])
+
+        load_hidden(0)
+        for gp in range(2):
+            for r in range(GROUP_HEADS):
+                nc.sync.dma_start(out=wk_raw[(gp, r)][:], in_=wk_rows[r][:, 1024 * gp : 1024 * (gp + 1)])
+        load_hidden(1)
+        nc.sync.dma_start(out=wq_raw[0][:], in_=wq_groups[0])
+        for i in range(2, 6):
+            load_hidden(i)
+
+        ident = const.tile([P, P], F32, name="ident")
+        make_identity(nc, ident[:])
+
+        token_i = const.tile([P, TOKEN_TILES], I32, name="token_i")
+        nc.gpsimd.iota(token_i[:], pattern=[[1, TOKEN_TILES]], base=0, channel_multiplier=TOKEN_TILES)
+        token = const.tile([P, TOKEN_TILES], F32, name="token")
+        nc.vector.tensor_copy(out=token[:], in_=token_i[:])
+
+        freq = const.tile([P, HALF], F32, name="freq")
+        nc.vector.memset(freq[:, 0:1], 1.0)
+        for m in (1, 2, 4, 8, 16, 32):
+            nc.vector.tensor_scalar(
+                out=freq[:, m : 2 * m], in0=freq[:, 0:m], scalar1=ROPE_BASE ** (-2.0 * m / D), scalar2=None, op0=ALU.mult
+            )
+        band = [j for j in range(HALF) if 0.0 < llama3_smooth(j) < 1.0]
+        for j in band:
+            nc.vector.tensor_scalar(
+                out=freq[:, j : j + 1], in0=freq[:, 0:1], scalar1=llama3_frequency(j), scalar2=None, op0=ALU.mult
+            )
+        low = band[-1] + 1
+        nc.vector.tensor_scalar(
+            out=freq[:, low:HALF], in0=freq[:, low:HALF], scalar1=1.0 / ROPE_FACTOR, scalar2=None, op0=ALU.mult
+        )
+
+        angle = const.tile([P, TOKEN_TILES, HALF], F32, name="angle")
+        nc.vector.tensor_tensor(
+            out=angle[:],
+            in0=token[:].unsqueeze(2).to_broadcast([P, TOKEN_TILES, HALF]),
+            in1=freq[:].unsqueeze(1).to_broadcast([P, TOKEN_TILES, HALF]),
+            op=ALU.mult,
+        )
+        angle_flat = angle[:].rearrange("p i j -> p (i j)")
+
+        reduced = {}
+        for name, quarter in (("sin", 0.0), ("cos", 0.25)):
+            turns_i = const.tile([P, TOKEN_TILES * HALF], I32, name="turns_i")
+            nc.vector.tensor_scalar(
+                out=turns_i[:], in0=angle_flat, scalar1=1.0 / TWO_PI, scalar2=quarter, op0=ALU.mult, op1=ALU.add
+            )
+            turns = const.tile([P, TOKEN_TILES * HALF], F32, name="turns")
+            nc.vector.tensor_copy(out=turns[:], in_=turns_i[:])
+            part = const.tile([P, TOKEN_TILES * HALF], F32, name="part")
+            nc.vector.scalar_tensor_tensor(
+                out=part[:], in0=turns[:], scalar=-TWO_PI_HIGH, in1=angle_flat, op0=ALU.mult, op1=ALU.add
+            )
+            rest = const.tile([P, TOKEN_TILES, HALF], F32, name="rest_" + name)
+            nc.vector.scalar_tensor_tensor(
+                out=rest[:].rearrange("p i j -> p (i j)"), in0=turns[:], scalar=-TWO_PI_LOW, in1=part[:], op0=ALU.mult, op1=ALU.add
+            )
+            reduced[name] = rest
+
+        table = const.tile([P, TOKEN_TILES, 2, 2, HALF], F32, name="table")
+
+        def fill_table():
+            nc.scalar.activation(out=table[:, :, 1, 0, :], in_=reduced["sin"][:], func=ACT.Sin)
+            nc.scalar.activation(out=table[:, :, 0, 0, :], in_=reduced["cos"][:], func=ACT.Sin, bias=PI / 2.0)
+            nc.vector.tensor_scalar(
+                out=table[:, :, 0, 1, :], in0=table[:, :, 1, 0, :], scalar1=-1.0, scalar2=None, op0=ALU.mult
+            )
+            nc.vector.tensor_copy(out=table[:, :, 1, 1, :], in_=table[:, :, 0, 0, :])
+
+        def transposes(words):
+            bank = psum_t.tile([P, 2, 2, P], F32, name="bank")
+            for gg in range(2):
+                for u in range(2):
+                    nc.tensor.transpose(bank[:, u, gg, :], words[:, 256 * gg + u : 256 * (gg + 1) : 2], ident[:])
+            return bank
+
+        def as_words(grouped, width):
+            return (
+                grouped[:]
+                .rearrange("p g n t -> p (g n t)")
+                .bitcast(F32)
+                .rearrange("p (g n u) -> p g n u", g=PASSES, n=width)
+            )
+
+        x_codes = {}
+        x_scales = {}
+        x_grouped = {}
+
+        def turn_hidden(i):
+            pair = i // 2
+            if i % 2 == 0:
+                x_grouped[pair] = groupedp.tile([P, 2, PASSES, P, 4], BF16, name="x_grouped", align_bytes=64)
+            words = (
+                x_grouped[pair][:, i % 2, :, :, :]
+                .rearrange("p g n t -> p (g n t)")
+                .bitcast(F32)
+                .rearrange("p (g n u) -> p g n u", g=PASSES, u=2)
+            )
+            for gp in range(2):
+                bank = transposes(x_raw[i][:, 1024 * gp : 1024 * (gp + 1)].bitcast(F32))
+                nc.scalar.copy(out=words[:, 2 * gp : 2 * gp + 2, :, :], in_=bank[:].rearrange("p u g n -> p g n u"))
+
+        def quantize_hidden(pair, first, count):
+            if pair not in x_codes:
+                x_codes[pair] = codes.tile([P, 2, PASSES * P], U32, name="x_codes%d" % pair, align_bytes=64)
+                x_scales[pair] = codes.tile([P, 2, PASSES * P], U8, name="x_scales%d" % pair, align_bytes=64)
+            tiles = slice(first, first + count)
+            nc.vector.quantize_mx(
+                out=x_codes[pair][:, tiles, :].rearrange("p i c -> p (i c)").bitcast(FP8X4),
+                scales=x_scales[pair][:, tiles, :].rearrange("p i c -> p (i c)"),
+                in_=x_grouped[pair][:, tiles, :, :, :].rearrange("p i g n t -> p (i g n t)"),
+            )
+
+        w_grouped = {}
+        w_codes = {}
+        w_scales = {}
+        wides = {}
+
+        def new_group(grp):
+            w_grouped[grp] = groupedp.tile([P, PASSES, N, 4], BF16, name="w_grouped", align_bytes=64)
+            w_codes[grp] = wcodes.tile([P, PASSES, N], U32, name="w_codes", align_bytes=64)
+            w_scales[grp] = wcodes.tile([P, PASSES, N], U8, name="w_scales", align_bytes=64)
+
+        def turn_wk(gp, r):
+            bank = transposes(wk_raw[(gp, r)][:].bitcast(F32))
+            target = as_words(w_grouped[0], N)[:, 2 * gp : 2 * gp + 2, P * r : P * (r + 1), :]
+            if r < 2:
+                nc.scalar.copy(out=target, in_=bank[:].rearrange("p u g n -> p g n u"))
+            else:
+                nc.vector.tensor_copy(out=target, in_=bank[:].rearrange("p u g n -> p g n u"))
+
+        def widen(grp, gp, r):
+            wides[(grp, gp, r)] = widep.tile([P, 1024], BF16, name="wide")
+            nc.scalar.copy(
+                out=wides[(grp, gp, r)][:], in_=wq_raw[grp - 1][:, r, 1024 * gp : 1024 * (gp + 1)].bitcast(FP8)
+            )
+
+        banks = {}
+
+        def turn_wq(grp, gp, r):
+            if gp == 0 and r == 0:
+                new_group(grp)
+            banks[(grp, gp, r)] = transposes(wides[(grp, gp, r)][:].bitcast(F32))
+
+        def scale_wq(grp, gp, r):
+            nc.vector.tensor_tensor(
+                out=w_grouped[grp][:, 2 * gp : 2 * gp + 2, P * r : P * (r + 1), :],
+                in0=banks[(grp, gp, r)][:]
+                .rearrange("p u g n -> p u (g n)")
+                .bitcast(BF16)
+                .rearrange("p u (m e) -> p m u e", e=2),
+                in1=scale4[:, 2 * gp : 2 * gp + 2, :].unsqueeze(2).to_broadcast([P, 2, P, 4]),
+                op=ALU.mult,
+            )
+
+        def quantize_weights(grp, gp):
+            passes = slice(2 * gp, 2 * gp + 2)
+            nc.vector.quantize_mx(
+                out=w_codes[grp][:, passes, :].rearrange("p g n -> p (g n)").bitcast(FP8X4),
+                scales=w_scales[grp][:, passes, :].rearrange("p g n -> p (g n)"),
+                in_=w_grouped[grp][:, passes, :, :].rearrange("p g n t -> p (g n t)"),
+            )
+
+        def project(grp, i):
+            acc = psum_a.tile([P, N], F32, name="acc")
+            for g in range(PASSES):
+                cols = slice(P * g, P * (g + 1))
+                nc.tensor.matmul_mx(
+                    out=acc[:],
+                    lhsT=x_codes[i // 2][:, i % 2, cols].bitcast(FP8X4),
+                    lhsT_scale=x_scales[i // 2][:, i % 2, cols],
+                    rhs=w_codes[grp][:, g, :].bitcast(FP8X4),
+                    rhs_scale=w_scales[grp][:, g, :],
+                    start=(g == 0),
+                    stop=(g == PASSES - 1),
+                )
+            return acc
+
+        def multiply(engine, source, products, i):
+            engine.tensor_tensor(
+                out=products[:, :, i % 2, :, :, :].rearrange("p h o s j -> p h o (s j)"),
+                in0=source[:].rearrange("p (h d) -> p h d", h=GROUP_HEADS).unsqueeze(2).to_broadcast([P, GROUP_HEADS, 2, D]),
+                in1=table[:, i, :, :, :].rearrange("p o s j -> p o (s j)").unsqueeze(1).to_broadcast([P, GROUP_HEADS, 2, D]),
+                op=ALU.mult,
+            )
+
+        turn_hidden(0)
+        quantize_hidden(0, 0, 1)
+        new_group(0)
+        for gp in range(2):
+            for r in range(GROUP_HEADS):
+                turn_wk(gp, r)
+            quantize_weights(0, gp)
+        fill_table()
+        turn_hidden(1)
+        quantize_hidden(0, 1, 1)
+        for i in range(6, TOKEN_TILES):
+            load_hidden(i)
+        for c in range(1, GROUPS - 1):
+            nc.sync.dma_start(out=wq_raw[c][:], in_=wq_groups[c])
+
+        wq_units = [(grp, gp, r) for grp in range(1, GROUPS) for gp in range(2) for r in range(GROUP_HEADS)]
+        for unit in wq_units[0:2]:
+            widen(*unit)
+        for step in range(GROUPS * TOKEN_TILES // 2):
+            grp = step // 4
+            i0 = 2 * (step % 4)
+            units = wq_units[2 * step : 2 * step + 2]
+            more_hidden = [i for i in (i0 + 2, i0 + 3) if grp == 0 and i < TOKEN_TILES]
+            sources = {}
+            if step == 0:
+                for i in (i0, i0 + 1):
+                    sources[i] = project(grp, i)
+            for unit in wq_units[2 * step + 2 : 2 * step + 4]:
+                widen(*unit)
+            for unit in units:
+                turn_wq(*unit)
+            for i in more_hidden:
+                turn_hidden(i)
+            if grp == 0 and step > 0:
+                for i in (i0, i0 + 1):
+                    sources[i] = project(grp, i)
+            for unit in units:
+                scale_wq(*unit)
+            if grp > 0:
+                for i in (i0, i0 + 1):
+                    sources[i] = project(grp, i)
+            for i in (i0, i0 + 1):
+                if i in OFFLOAD[grp]:
+                    staged = stagep.tile([P, N], F32, name="staged")
+                    nc.scalar.copy(out=staged[:], in_=sources[i][:])
+                    sources[i] = staged
+            products = ropep.tile([P, GROUP_HEADS, 2, 2, 2, HALF], F32, name="products")
+            for i in (i0, i0 + 1):
+                multiply(nc.gpsimd if i in OFFLOAD[grp] else nc.vector, sources[i], products, i)
+            if units and units[1][2] == GROUP_HEADS - 1:
+                quantize_weights(units[1][0], units[1][1])
+            result = ropep.tile([P, GROUP_HEADS, 2, D], F32, name="result")
+            adder = nc.vector if (grp, i0) in VECTOR_ADDS else nc.gpsimd
+            adder.tensor_tensor(
+                out=result[:].rearrange("p h i (o j) -> p (h i o) j", o=2),
+                in0=products[:, :, :, :, 0, :].rearrange("p h i o j -> p (h i o) j"),
+                in1=products[:, :, :, :, 1, :].rearrange("p h i o j -> p (h i o) j"),
+                op=ALU.add,
+            )
+            if more_hidden:
+                quantize_hidden(more_hidden[0] // 2, 0, 2)
+            if grp == 0:
+                target = k_view[:, :, i0 : i0 + 2, :]
+            else:
+                target = q_view[:, GROUP_HEADS * (grp - 1) : GROUP_HEADS * grp, i0 : i0 + 2, :]
+            nc.sync.dma_start(out=target, in_=result[:])

@@ -33,7 +33,6 @@ TWO_PI = 2.0 * PI
 TWO_PI_HIGH = 6.28125
 TWO_PI_LOW = TWO_PI - TWO_PI_HIGH
 
-OFFLOAD = {0: (1, 3, 5), 1: (1, 5), 2: (1, 3, 5), 3: (1, 5), 4: ()}
 VECTOR_ADDS = ((4, 6),)
 
 
@@ -53,20 +52,20 @@ def tile_stickyllamaattention_pa_kernel(tc, hidden_states, wq_bytes, wq_scale, w
 
     hidden_tiles = hidden_states.rearrange("o (p i) k -> i p (o k)", i=TOKEN_TILES)
     wk_rows = wk.rearrange("(r p) k -> r p k", p=P)
-    wq_groups = wq_bytes.rearrange("(c r p) k -> c p r k", r=GROUP_HEADS, p=P)
+    wq_halves = wq_bytes.rearrange("(c r p) (gp k) -> c gp p r k", r=GROUP_HEADS, p=P, gp=2)
     q_view = out_0.rearrange("o h (p i) d -> p (o h) i d", i=TOKEN_TILES)
     k_view = out_1.rearrange("o h (p i) d -> p (o h) i d", i=TOKEN_TILES)
 
     with ExitStack() as ctx:
         const = ctx.enter_context(tc.tile_pool(name="const", bufs=1))
         raw = ctx.enter_context(tc.tile_pool(name="raw", bufs=1))
-        xpool = ctx.enter_context(tc.tile_pool(name="xpool", bufs=6))
-        widep = ctx.enter_context(tc.tile_pool(name="widep", bufs=4))
+        xpool = ctx.enter_context(tc.tile_pool(name="xpool", bufs=4))
+        widep = ctx.enter_context(tc.tile_pool(name="widep", bufs=8))
+        planesp = ctx.enter_context(tc.tile_pool(name="planesp", bufs=2))
         groupedp = ctx.enter_context(tc.tile_pool(name="groupedp", bufs=2))
         codes = ctx.enter_context(tc.tile_pool(name="codes", bufs=1))
         wcodes = ctx.enter_context(tc.tile_pool(name="wcodes", bufs=2))
         ropep = ctx.enter_context(tc.tile_pool(name="ropep", bufs=3))
-        stagep = ctx.enter_context(tc.tile_pool(name="stagep", bufs=2))
         psum_t = ctx.enter_context(tc.psum_pool(name="psum_t", bufs=4))
         psum_a = ctx.enter_context(tc.psum_pool(name="psum_a", bufs=4))
 
@@ -76,9 +75,13 @@ def tile_stickyllamaattention_pa_kernel(tc, hidden_states, wq_bytes, wq_scale, w
 
         scale4 = const.tile([P, PASSES, 4], F32, name="scale4")
         nc.scalar.dma_start(out=scale4[:], in_=wq_scale.rearrange("o (g p t) -> p (o g) t", p=P, t=4))
-        wq_raw = []
+        wq_raw = {}
         for c in range(GROUPS - 1):
-            wq_raw.append(raw.tile([P, GROUP_HEADS, H], U8, name="wq_raw%d" % c))
+            for gp in range(2):
+                wq_raw[(c, gp)] = raw.tile([P, GROUP_HEADS, H // 2], U8, name="wq_raw%d_%d" % (c, gp))
+
+        def load_wq(c, gp):
+            nc.sync.dma_start(out=wq_raw[(c, gp)][:], in_=wq_halves[c][gp])
         wk_raw = {}
         for gp in range(2):
             for r in range(GROUP_HEADS):
@@ -90,12 +93,13 @@ def tile_stickyllamaattention_pa_kernel(tc, hidden_states, wq_bytes, wq_scale, w
             nc.sync.dma_start(out=x_raw[i][:], in_=hidden_tiles[i])
 
         load_hidden(0)
+        load_wq(0, 0)
         for gp in range(2):
             for r in range(GROUP_HEADS):
                 nc.sync.dma_start(out=wk_raw[(gp, r)][:], in_=wk_rows[r][:, 1024 * gp : 1024 * (gp + 1)])
         load_hidden(1)
-        nc.sync.dma_start(out=wq_raw[0][:], in_=wq_groups[0])
-        for i in range(2, 6):
+        load_wq(0, 1)
+        for i in range(2, 4):
             load_hidden(i)
 
         ident = const.tile([P, P], F32, name="ident")
@@ -216,22 +220,17 @@ def tile_stickyllamaattention_pa_kernel(tc, hidden_states, wq_bytes, wq_scale, w
         def turn_wk(gp, r):
             bank = transposes(wk_raw[(gp, r)][:].bitcast(F32))
             target = as_words(w_grouped[0], N)[:, 2 * gp : 2 * gp + 2, P * r : P * (r + 1), :]
-            if r < 2:
-                nc.scalar.copy(out=target, in_=bank[:].rearrange("p u g n -> p g n u"))
-            else:
-                nc.vector.tensor_copy(out=target, in_=bank[:].rearrange("p u g n -> p g n u"))
+            nc.vector.tensor_copy(out=target, in_=bank[:].rearrange("p u g n -> p g n u"))
 
         def widen(grp, gp, r):
             wides[(grp, gp, r)] = widep.tile([P, 1024], BF16, name="wide")
             nc.scalar.copy(
-                out=wides[(grp, gp, r)][:], in_=wq_raw[grp - 1][:, r, 1024 * gp : 1024 * (gp + 1)].bitcast(FP8)
+                out=wides[(grp, gp, r)][:], in_=wq_raw[(grp - 1, gp)][:, r, :].bitcast(FP8)
             )
 
         banks = {}
 
         def turn_wq(grp, gp, r):
-            if gp == 0 and r == 0:
-                new_group(grp)
             banks[(grp, gp, r)] = transposes(wides[(grp, gp, r)][:].bitcast(F32))
 
         def scale_wq(grp, gp, r):
@@ -276,8 +275,55 @@ def tile_stickyllamaattention_pa_kernel(tc, hidden_states, wq_bytes, wq_scale, w
                 op=ALU.mult,
             )
 
+        pass_banks = {}
+        planes = {}
+
+        def turn_pass(grp, g):
+            if g == 0:
+                new_group(grp)
+            for u in range(2):
+                pass_banks[(grp, g, u)] = psum_t.tile([P, GROUP_HEADS, P], F32, name="bank")
+            for r in range(GROUP_HEADS):
+                words = wides[(grp, g // 2, r)][:].bitcast(F32)
+                for u in range(2):
+                    nc.tensor.transpose(
+                        pass_banks[(grp, g, u)][:, r, :], words[:, 256 * (g % 2) + u : 256 * (g % 2 + 1) : 2], ident[:]
+                    )
+
+        def scale_pass(grp, g):
+            planes[(grp, g)] = planesp.tile([P, 4, N], BF16, name="planes")
+            for u in range(2):
+                pairs = (
+                    pass_banks[(grp, g, u)][:]
+                    .rearrange("p r n -> p (r n)")
+                    .bitcast(BF16)
+                    .rearrange("p (m e) -> p m e", e=2)
+                )
+                for e in range(2):
+                    t = 2 * u + e
+                    nc.scalar.activation(
+                        out=planes[(grp, g)][:, t, :], in_=pairs[:, :, e], func=ACT.Copy, scale=scale4[:, g, t : t + 1]
+                    )
+
+        def interleave_pass(grp, g):
+            nc.gpsimd.tensor_scalar(
+                out=w_grouped[grp][:, g, :, :],
+                in0=planes[(grp, g)][:].rearrange("p t n -> p n t"),
+                scalar1=1.0,
+                scalar2=0.0,
+                op0=ALU.mult,
+                op1=ALU.add,
+            )
+
         turn_hidden(0)
         quantize_hidden(0, 0, 1)
+        load_hidden(4)
+        for r in range(GROUP_HEADS):
+            widen(1, 0, r)
+        for g in range(2):
+            turn_pass(1, g)
+            scale_pass(1, g)
+            interleave_pass(1, g)
         new_group(0)
         for gp in range(2):
             for r in range(GROUP_HEADS):
@@ -286,47 +332,55 @@ def tile_stickyllamaattention_pa_kernel(tc, hidden_states, wq_bytes, wq_scale, w
         fill_table()
         turn_hidden(1)
         quantize_hidden(0, 1, 1)
-        for i in range(6, TOKEN_TILES):
-            load_hidden(i)
+        load_hidden(5)
+        widen(1, 1, 0)
         for c in range(1, GROUPS - 1):
-            nc.sync.dma_start(out=wq_raw[c][:], in_=wq_groups[c])
+            for gp in range(2):
+                load_wq(c, gp)
 
-        wq_units = [(grp, gp, r) for grp in range(1, GROUPS) for gp in range(2) for r in range(GROUP_HEADS)]
-        for unit in wq_units[0:2]:
-            widen(*unit)
         for step in range(GROUPS * TOKEN_TILES // 2):
-            grp = step // 4
-            i0 = 2 * (step % 4)
-            units = wq_units[2 * step : 2 * step + 2]
+            grp, s = divmod(step, 4)
+            i0 = 2 * s
+            nxt = grp + 1
             more_hidden = [i for i in (i0 + 2, i0 + 3) if grp == 0 and i < TOKEN_TILES]
             sources = {}
             if step == 0:
                 for i in (i0, i0 + 1):
                     sources[i] = project(grp, i)
-            for unit in wq_units[2 * step + 2 : 2 * step + 4]:
-                widen(*unit)
-            for unit in units:
-                turn_wq(*unit)
+            if nxt < GROUPS and s < 3:
+                widen(nxt, 1, s + 1)
+            if nxt + 1 < GROUPS and s >= 2:
+                widen(nxt + 1, 0, 2 * s - 4)
+                widen(nxt + 1, 0, 2 * s - 3)
+            if nxt + 1 < GROUPS and s == 3:
+                widen(nxt + 1, 1, 0)
+            if nxt < GROUPS:
+                if s < 2 and nxt > 1:
+                    turn_pass(nxt, s)
+                turn_wq(nxt, 1, s)
             for i in more_hidden:
                 turn_hidden(i)
+                if i + 4 < TOKEN_TILES:
+                    load_hidden(i + 4)
             if grp == 0 and step > 0:
                 for i in (i0, i0 + 1):
                     sources[i] = project(grp, i)
-            for unit in units:
-                scale_wq(*unit)
+            if nxt < GROUPS:
+                if s < 2 and nxt > 1:
+                    scale_pass(nxt, s)
+                if 1 <= s <= 2 and nxt > 1:
+                    interleave_pass(nxt, s - 1)
+                scale_wq(nxt, 1, s)
+                if s == (3 if nxt > 1 else 0):
+                    quantize_weights(nxt, 0)
             if grp > 0:
                 for i in (i0, i0 + 1):
                     sources[i] = project(grp, i)
-            for i in (i0, i0 + 1):
-                if i in OFFLOAD[grp]:
-                    staged = stagep.tile([P, N], F32, name="staged")
-                    nc.scalar.copy(out=staged[:], in_=sources[i][:])
-                    sources[i] = staged
             products = ropep.tile([P, GROUP_HEADS, 2, 2, 2, HALF], F32, name="products")
             for i in (i0, i0 + 1):
-                multiply(nc.gpsimd if i in OFFLOAD[grp] else nc.vector, sources[i], products, i)
-            if units and units[1][2] == GROUP_HEADS - 1:
-                quantize_weights(units[1][0], units[1][1])
+                multiply(nc.vector, sources[i], products, i)
+            if nxt < GROUPS and s == 3:
+                quantize_weights(nxt, 1)
             result = ropep.tile([P, GROUP_HEADS, 2, D], F32, name="result")
             adder = nc.vector if (grp, i0) in VECTOR_ADDS else nc.gpsimd
             adder.tensor_tensor(

@@ -34,6 +34,7 @@ TWO_PI_HIGH = 6.28125
 TWO_PI_LOW = TWO_PI - TWO_PI_HIGH
 
 VECTOR_ADDS = ((4, 6),)
+OFFLOAD = {0: (3,), 1: (5,), 2: (5,), 3: (5,), 4: (1,)}
 
 
 def llama3_smooth(j):
@@ -66,6 +67,7 @@ def tile_stickyllamaattention_pa_kernel(tc, hidden_states, wq_bytes, wq_scale, w
         codes = ctx.enter_context(tc.tile_pool(name="codes", bufs=1))
         wcodes = ctx.enter_context(tc.tile_pool(name="wcodes", bufs=2))
         ropep = ctx.enter_context(tc.tile_pool(name="ropep", bufs=3))
+        stagep = ctx.enter_context(tc.tile_pool(name="stagep", bufs=1))
         psum_t = ctx.enter_context(tc.psum_pool(name="psum_t", bufs=4))
         psum_a = ctx.enter_context(tc.psum_pool(name="psum_a", bufs=4))
 
@@ -306,6 +308,9 @@ def tile_stickyllamaattention_pa_kernel(tc, hidden_states, wq_bytes, wq_scale, w
                     )
 
         def interleave_pass(grp, g):
+            if grp > 1 and g == 1:
+                nc.scalar.copy(out=w_grouped[grp][:, g, :, :], in_=planes[(grp, g)][:].rearrange("p t n -> p n t"))
+                return
             nc.gpsimd.tensor_scalar(
                 out=w_grouped[grp][:, g, :, :],
                 in0=planes[(grp, g)][:].rearrange("p t n -> p n t"),
@@ -378,7 +383,12 @@ def tile_stickyllamaattention_pa_kernel(tc, hidden_states, wq_bytes, wq_scale, w
                     sources[i] = project(grp, i)
             products = ropep.tile([P, GROUP_HEADS, 2, 2, 2, HALF], F32, name="products")
             for i in (i0, i0 + 1):
-                multiply(nc.vector, sources[i], products, i)
+                if i in OFFLOAD[grp]:
+                    staged = stagep.tile([P, N], F32, name="staged")
+                    nc.scalar.copy(out=staged[:], in_=sources[i][:])
+                    sources[i] = staged
+            for i in (i0, i0 + 1):
+                multiply(nc.gpsimd if i in OFFLOAD[grp] else nc.vector, sources[i], products, i)
             if nxt < GROUPS and s == 3:
                 quantize_weights(nxt, 1)
             result = ropep.tile([P, GROUP_HEADS, 2, D], F32, name="result")

@@ -33,8 +33,15 @@ TWO_PI = 2.0 * PI
 TWO_PI_HIGH = 6.28125
 TWO_PI_LOW = TWO_PI - TWO_PI_HIGH
 
-VECTOR_ADDS = ((4, 6),)
-OFFLOAD = {0: (3,), 1: (5,), 2: (5,), 3: (5,), 4: (1,)}
+V_ADDS = (19,)
+OFFLOAD = ()
+WK_SCALAR = ((0, 1), (0, 3), (1, 1), (1, 3))
+WIDEN = ((8, 0, (0, 1)), (7, 0, (2, 3)), (7, 1, (0,)), (6, 1, (1,)), (5, 1, (2,)), (4, 1, (3,)))
+SPASS = ((5, 0), (4, 1))
+UNITS = ((5, 1, 0), (4, 1, 1), (3, 1, 2), (2, 1, 3))
+UNITS1 = ((5, 0, 0), (5, 0, 1), (4, 0, 2), (4, 0, 3), (3, 1, 0), (3, 1, 1), (2, 1, 2), (2, 1, 3))
+INTER = ((4, 0, "G"), (3, 1, "S"))
+QUANT = ((3, 0), (2, 1))
 
 
 def llama3_smooth(j):
@@ -60,15 +67,18 @@ def tile_stickyllamaattention_pa_kernel(tc, hidden_states, wq_bytes, wq_scale, w
     with ExitStack() as ctx:
         const = ctx.enter_context(tc.tile_pool(name="const", bufs=1))
         raw = ctx.enter_context(tc.tile_pool(name="raw", bufs=1))
-        xpool = ctx.enter_context(tc.tile_pool(name="xpool", bufs=4))
+        xpool = ctx.enter_context(tc.tile_pool(name="xpool", bufs=8))
+        wqpool = ctx.enter_context(tc.tile_pool(name="wqpool", bufs=4))
         widep = ctx.enter_context(tc.tile_pool(name="widep", bufs=8))
         planesp = ctx.enter_context(tc.tile_pool(name="planesp", bufs=2))
         groupedp = ctx.enter_context(tc.tile_pool(name="groupedp", bufs=2))
         codes = ctx.enter_context(tc.tile_pool(name="codes", bufs=1))
         wcodes = ctx.enter_context(tc.tile_pool(name="wcodes", bufs=2))
         ropep = ctx.enter_context(tc.tile_pool(name="ropep", bufs=3))
+        resultp = ctx.enter_context(tc.tile_pool(name="resultp", bufs=4))
         stagep = ctx.enter_context(tc.tile_pool(name="stagep", bufs=1))
-        psum_t = ctx.enter_context(tc.psum_pool(name="psum_t", bufs=4))
+        psum_v = ctx.enter_context(tc.psum_pool(name="psum_v", bufs=2))
+        psum_s = ctx.enter_context(tc.psum_pool(name="psum_s", bufs=2))
         psum_a = ctx.enter_context(tc.psum_pool(name="psum_a", bufs=4))
 
         warm = const.tile([P, 2], F32, name="warm")
@@ -78,11 +88,13 @@ def tile_stickyllamaattention_pa_kernel(tc, hidden_states, wq_bytes, wq_scale, w
         scale4 = const.tile([P, PASSES, 4], F32, name="scale4")
         nc.scalar.dma_start(out=scale4[:], in_=wq_scale.rearrange("o (g p t) -> p (o g) t", p=P, t=4))
         wq_raw = {}
-        for c in range(GROUPS - 1):
+
+        def load_wq_all(c):
             for gp in range(2):
-                wq_raw[(c, gp)] = raw.tile([P, GROUP_HEADS, H // 2], U8, name="wq_raw%d_%d" % (c, gp))
+                load_wq(c, gp)
 
         def load_wq(c, gp):
+            wq_raw[(c, gp)] = wqpool.tile([P, GROUP_HEADS, H // 2], U8, name="wq_raw")
             nc.sync.dma_start(out=wq_raw[(c, gp)][:], in_=wq_halves[c][gp])
         wk_raw = {}
         for gp in range(2):
@@ -94,15 +106,21 @@ def tile_stickyllamaattention_pa_kernel(tc, hidden_states, wq_bytes, wq_scale, w
             x_raw[i] = xpool.tile([P, H], BF16, name="x_raw")
             nc.sync.dma_start(out=x_raw[i][:], in_=hidden_tiles[i])
 
-        load_hidden(0)
-        load_wq(0, 0)
-        for gp in range(2):
+        def load_wk(gp):
             for r in range(GROUP_HEADS):
                 nc.sync.dma_start(out=wk_raw[(gp, r)][:], in_=wk_rows[r][:, 1024 * gp : 1024 * (gp + 1)])
+
+        load_hidden(0)
+        load_wk(0)
         load_hidden(1)
+        load_wk(1)
+        load_wq(0, 0)
+        load_hidden(2)
+        load_hidden(3)
         load_wq(0, 1)
-        for i in range(2, 4):
+        for i in range(4, TOKEN_TILES):
             load_hidden(i)
+        load_wq_all(1)
 
         ident = const.tile([P, P], F32, name="ident")
         make_identity(nc, ident[:])
@@ -138,7 +156,7 @@ def tile_stickyllamaattention_pa_kernel(tc, hidden_states, wq_bytes, wq_scale, w
         angle_flat = angle[:].rearrange("p i j -> p (i j)")
 
         reduced = {}
-        for name, quarter in (("sin", 0.0), ("cos", 0.25)):
+        for name, quarter in (("sin", 0.0),):
             turns_i = const.tile([P, TOKEN_TILES * HALF], I32, name="turns_i")
             nc.vector.tensor_scalar(
                 out=turns_i[:], in0=angle_flat, scalar1=1.0 / TWO_PI, scalar2=quarter, op0=ALU.mult, op1=ALU.add
@@ -157,16 +175,23 @@ def tile_stickyllamaattention_pa_kernel(tc, hidden_states, wq_bytes, wq_scale, w
 
         table = const.tile([P, TOKEN_TILES, 2, 2, HALF], F32, name="table")
 
-        def fill_table():
-            nc.scalar.activation(out=table[:, :, 1, 0, :], in_=reduced["sin"][:], func=ACT.Sin)
-            nc.scalar.activation(out=table[:, :, 0, 0, :], in_=reduced["cos"][:], func=ACT.Sin, bias=PI / 2.0)
-            nc.vector.tensor_scalar(
-                out=table[:, :, 0, 1, :], in0=table[:, :, 1, 0, :], scalar1=-1.0, scalar2=None, op0=ALU.mult
-            )
-            nc.vector.tensor_copy(out=table[:, :, 1, 1, :], in_=table[:, :, 0, 0, :])
+        half_sin = const.tile([P, TOKEN_TILES, HALF], F32, name="turns")
+        square = const.tile([P, TOKEN_TILES, HALF], F32, name="part")
 
-        def transposes(words):
-            bank = psum_t.tile([P, 2, 2, P], F32, name="bank")
+        def fill_table():
+            nc.scalar.activation(out=half_sin[:], in_=reduced["sin"][:], func=ACT.Sin, scale=0.5)
+            nc.scalar.activation(out=table[:, :, 1, 0, :], in_=reduced["sin"][:], func=ACT.Sin)
+            nc.gpsimd.tensor_tensor(out=square[:], in0=half_sin[:], in1=half_sin[:], op=ALU.mult)
+            for half in range(2):
+                nc.gpsimd.tensor_scalar(
+                    out=table[:, :, half, half, :], in0=square[:], scalar1=-2.0, scalar2=1.0, op0=ALU.mult, op1=ALU.add
+                )
+            nc.gpsimd.tensor_scalar(
+                out=table[:, :, 0, 1, :], in0=table[:, :, 1, 0, :], scalar1=-1.0, scalar2=0.0, op0=ALU.mult, op1=ALU.add
+            )
+
+        def transposes(words, pool):
+            bank = pool.tile([P, 2, 2, P], F32, name="bank")
             for gg in range(2):
                 for u in range(2):
                     nc.tensor.transpose(bank[:, u, gg, :], words[:, 256 * gg + u : 256 * (gg + 1) : 2], ident[:])
@@ -195,7 +220,7 @@ def tile_stickyllamaattention_pa_kernel(tc, hidden_states, wq_bytes, wq_scale, w
                 .rearrange("p (g n u) -> p g n u", g=PASSES, u=2)
             )
             for gp in range(2):
-                bank = transposes(x_raw[i][:, 1024 * gp : 1024 * (gp + 1)].bitcast(F32))
+                bank = transposes(x_raw[i][:, 1024 * gp : 1024 * (gp + 1)].bitcast(F32), psum_s)
                 nc.scalar.copy(out=words[:, 2 * gp : 2 * gp + 2, :, :], in_=bank[:].rearrange("p u g n -> p g n u"))
 
         def quantize_hidden(pair, first, count):
@@ -219,10 +244,15 @@ def tile_stickyllamaattention_pa_kernel(tc, hidden_states, wq_bytes, wq_scale, w
             w_codes[grp] = wcodes.tile([P, PASSES, N], U32, name="w_codes", align_bytes=64)
             w_scales[grp] = wcodes.tile([P, PASSES, N], U8, name="w_scales", align_bytes=64)
 
-        def turn_wk(gp, r):
-            bank = transposes(wk_raw[(gp, r)][:].bitcast(F32))
+        def bank_of_wk(gp, r):
+            if (gp, r) == (0, 0):
+                new_group(0)
+            bank = transposes(wk_raw[(gp, r)][:].bitcast(F32), psum_v)
             target = as_words(w_grouped[0], N)[:, 2 * gp : 2 * gp + 2, P * r : P * (r + 1), :]
-            nc.vector.tensor_copy(out=target, in_=bank[:].rearrange("p u g n -> p g n u"))
+            if (gp, r) in WK_SCALAR:
+                nc.scalar.copy(out=target, in_=bank[:].rearrange("p u g n -> p g n u"))
+            else:
+                nc.vector.tensor_copy(out=target, in_=bank[:].rearrange("p u g n -> p g n u"))
 
         def widen(grp, gp, r):
             wides[(grp, gp, r)] = widep.tile([P, 1024], BF16, name="wide")
@@ -233,12 +263,30 @@ def tile_stickyllamaattention_pa_kernel(tc, hidden_states, wq_bytes, wq_scale, w
         banks = {}
 
         def turn_wq(grp, gp, r):
-            banks[(grp, gp, r)] = transposes(wides[(grp, gp, r)][:].bitcast(F32))
+            banks[(grp, gp, r)] = transposes(wides[(grp, gp, r)][:].bitcast(F32), psum_v)
 
         def scale_wq(grp, gp, r):
             nc.vector.tensor_tensor(
                 out=w_grouped[grp][:, 2 * gp : 2 * gp + 2, P * r : P * (r + 1), :],
                 in0=banks[(grp, gp, r)][:]
+                .rearrange("p u g n -> p u (g n)")
+                .bitcast(BF16)
+                .rearrange("p u (m e) -> p m u e", e=2),
+                in1=scale4[:, 2 * gp : 2 * gp + 2, :].unsqueeze(2).to_broadcast([P, 2, P, 4]),
+                op=ALU.mult,
+            )
+
+        unit_banks = {}
+
+        def turn_unit(grp, gp, r):
+            if grp not in w_grouped:
+                new_group(grp)
+            unit_banks[(grp, gp, r)] = transposes(wides[(grp, gp, r)][:].bitcast(F32), psum_v)
+
+        def scale_unit(grp, gp, r):
+            nc.vector.tensor_tensor(
+                out=w_grouped[grp][:, 2 * gp : 2 * gp + 2, P * r : P * (r + 1), :],
+                in0=unit_banks[(grp, gp, r)][:]
                 .rearrange("p u g n -> p u (g n)")
                 .bitcast(BF16)
                 .rearrange("p u (m e) -> p m u e", e=2),
@@ -281,10 +329,10 @@ def tile_stickyllamaattention_pa_kernel(tc, hidden_states, wq_bytes, wq_scale, w
         planes = {}
 
         def turn_pass(grp, g):
-            if g == 0:
+            if grp not in w_grouped:
                 new_group(grp)
             for u in range(2):
-                pass_banks[(grp, g, u)] = psum_t.tile([P, GROUP_HEADS, P], F32, name="bank")
+                pass_banks[(grp, g, u)] = psum_s.tile([P, GROUP_HEADS, P], F32, name="bank")
             for r in range(GROUP_HEADS):
                 words = wides[(grp, g // 2, r)][:].bitcast(F32)
                 for u in range(2):
@@ -307,8 +355,8 @@ def tile_stickyllamaattention_pa_kernel(tc, hidden_states, wq_bytes, wq_scale, w
                         out=planes[(grp, g)][:, t, :], in_=pairs[:, :, e], func=ACT.Copy, scale=scale4[:, g, t : t + 1]
                     )
 
-        def interleave_pass(grp, g):
-            if grp > 1 and g == 1:
+        def interleave_pass(grp, g, engine):
+            if engine == "S":
                 nc.scalar.copy(out=w_grouped[grp][:, g, :, :], in_=planes[(grp, g)][:].rearrange("p t n -> p n t"))
                 return
             nc.gpsimd.tensor_scalar(
@@ -320,89 +368,130 @@ def tile_stickyllamaattention_pa_kernel(tc, hidden_states, wq_bytes, wq_scale, w
                 op1=ALU.add,
             )
 
-        turn_hidden(0)
-        quantize_hidden(0, 0, 1)
-        load_hidden(4)
-        for r in range(GROUP_HEADS):
-            widen(1, 0, r)
-        for g in range(2):
-            turn_pass(1, g)
-            scale_pass(1, g)
-            interleave_pass(1, g)
-        new_group(0)
-        for gp in range(2):
-            for r in range(GROUP_HEADS):
-                turn_wk(gp, r)
-            quantize_weights(0, gp)
-        fill_table()
-        turn_hidden(1)
-        quantize_hidden(0, 1, 1)
-        load_hidden(5)
-        widen(1, 1, 0)
-        for c in range(1, GROUPS - 1):
-            for gp in range(2):
-                load_wq(c, gp)
+        ctx.enter_context(tc.manual_schedule(engines={mybir.EngineType.DVE}))
+        STEPS = GROUPS * TOKEN_TILES // 2
 
-        for step in range(GROUPS * TOKEN_TILES // 2):
-            grp, s = divmod(step, 4)
-            i0 = 2 * s
-            nxt = grp + 1
-            more_hidden = [i for i in (i0 + 2, i0 + 3) if grp == 0 and i < TOKEN_TILES]
-            sources = {}
-            if step == 0:
-                for i in (i0, i0 + 1):
-                    sources[i] = project(grp, i)
-            if nxt < GROUPS and s < 3:
-                widen(nxt, 1, s + 1)
-            if nxt + 1 < GROUPS and s >= 2:
-                widen(nxt + 1, 0, 2 * s - 4)
-                widen(nxt + 1, 0, 2 * s - 3)
-            if nxt + 1 < GROUPS and s == 3:
-                widen(nxt + 1, 1, 0)
-            if nxt < GROUPS:
-                if s < 2 and nxt > 1:
-                    turn_pass(nxt, s)
-                turn_wq(nxt, 1, s)
-            for i in more_hidden:
-                turn_hidden(i)
-                if i + 4 < TOKEN_TILES:
-                    load_hidden(i + 4)
-            if grp == 0 and step > 0:
-                for i in (i0, i0 + 1):
-                    sources[i] = project(grp, i)
-            if nxt < GROUPS:
-                if s < 2 and nxt > 1:
-                    scale_pass(nxt, s)
-                if 1 <= s <= 2 and nxt > 1:
-                    interleave_pass(nxt, s - 1)
-                scale_wq(nxt, 1, s)
-                if s == (3 if nxt > 1 else 0):
-                    quantize_weights(nxt, 0)
-            if grp > 0:
-                for i in (i0, i0 + 1):
-                    sources[i] = project(grp, i)
-            products = ropep.tile([P, GROUP_HEADS, 2, 2, 2, HALF], F32, name="products")
-            for i in (i0, i0 + 1):
-                if i in OFFLOAD[grp]:
-                    staged = stagep.tile([P, N], F32, name="staged")
-                    nc.scalar.copy(out=staged[:], in_=sources[i][:])
-                    sources[i] = staged
-            for i in (i0, i0 + 1):
-                multiply(nc.gpsimd if i in OFFLOAD[grp] else nc.vector, sources[i], products, i)
-            if nxt < GROUPS and s == 3:
-                quantize_weights(nxt, 1)
-            result = ropep.tile([P, GROUP_HEADS, 2, D], F32, name="result")
-            adder = nc.vector if (grp, i0) in VECTOR_ADDS else nc.gpsimd
-            adder.tensor_tensor(
+        def add_pair(engine, grp, products, i0):
+            result = resultp.tile([P, GROUP_HEADS, 2, D], F32, name="result")
+            engine.tensor_tensor(
                 out=result[:].rearrange("p h i (o j) -> p (h i o) j", o=2),
                 in0=products[:, :, :, :, 0, :].rearrange("p h i o j -> p (h i o) j"),
                 in1=products[:, :, :, :, 1, :].rearrange("p h i o j -> p (h i o) j"),
                 op=ALU.add,
             )
-            if more_hidden:
-                quantize_hidden(more_hidden[0] // 2, 0, 2)
             if grp == 0:
                 target = k_view[:, :, i0 : i0 + 2, :]
             else:
                 target = q_view[:, GROUP_HEADS * (grp - 1) : GROUP_HEADS * grp, i0 : i0 + 2, :]
             nc.sync.dma_start(out=target, in_=result[:])
+
+        sources = {}
+
+        def project_step(b):
+            if b < STEPS:
+                for i in (2 * (b % 4), 2 * (b % 4) + 1):
+                    sources[(b, i)] = project(b // 4, i)
+
+        def due(a, lead):
+            nxt, rest = divmod(a + lead, 4)
+            return nxt if rest == 0 and 1 <= nxt < GROUPS else None
+
+        def do_widen(a):
+            for lead, gp, rows in WIDEN:
+                nxt = due(a, lead)
+                if nxt and nxt > 1:
+                    for r in rows:
+                        widen(nxt, gp, r)
+
+        def feed_units(a):
+            for nxt in range(1, GROUPS):
+                for lead, gp, r in UNITS1 if nxt == 1 else UNITS:
+                    if 4 * nxt - a == lead:
+                        turn_unit(nxt, gp, r)
+
+        def feed_passes(a):
+            for lead, g in SPASS:
+                nxt = due(a, lead)
+                if nxt and nxt > 1:
+                    turn_pass(nxt, g)
+
+        def do_passes(a):
+            for lead, g in SPASS:
+                nxt = due(a, lead)
+                if nxt and nxt > 1:
+                    scale_pass(nxt, g)
+
+        def do_units(a):
+            for nxt in range(1, GROUPS):
+                for lead, gp, r in UNITS1 if nxt == 1 else UNITS:
+                    if 4 * nxt - a == lead:
+                        scale_unit(nxt, gp, r)
+
+        def do_inter(a, engine):
+            for lead, g, e in INTER:
+                nxt = due(a, lead)
+                if nxt and nxt > 1:
+                    if e == engine:
+                        interleave_pass(nxt, g, e)
+
+        def do_quant(a):
+            for lead, gp in QUANT:
+                nxt = due(a, lead)
+                if nxt:
+                    quantize_weights(nxt, gp)
+
+        turn_hidden(0)
+        for r in range(GROUP_HEADS):
+            bank_of_wk(0, r)
+        fill_table()
+        turn_hidden(1)
+        quantize_weights(0, 0)
+        for r in range(GROUP_HEADS):
+            bank_of_wk(1, r)
+        quantize_hidden(0, 0, 2)
+        quantize_weights(0, 1)
+        for r in range(2):
+            widen(1, 0, r)
+        feed_units(-1)
+        project_step(0)
+        turn_hidden(2)
+        turn_hidden(3)
+        for r in range(2, 4):
+            widen(1, 0, r)
+        do_units(-1)
+        feed_units(0)
+        quantize_hidden(1, 0, 2)
+        turn_hidden(4)
+        turn_hidden(5)
+
+        for a in range(STEPS):
+            grp, st = divmod(a, 4)
+            i0 = 2 * st
+            do_passes(a)
+            project_step(a + 1)
+            if a == 0:
+                turn_hidden(6)
+                turn_hidden(7)
+                for r in range(GROUP_HEADS):
+                    widen(1, 1, r)
+            do_units(a)
+            feed_units(a + 1)
+            do_inter(a, "S")
+            do_widen(a)
+            feed_passes(a + 1)
+            products = ropep.tile([P, GROUP_HEADS, 2, 2, 2, HALF], F32, name="products")
+            for i in (i0, i0 + 1):
+                if (grp, i) in OFFLOAD:
+                    staged = stagep.tile([P, N], F32, name="staged")
+                    nc.scalar.copy(out=staged[:], in_=sources[(a, i)][:])
+                    multiply(nc.gpsimd, staged, products, i)
+            for i in (i0, i0 + 1):
+                if (grp, i) not in OFFLOAD:
+                    multiply(nc.vector, sources[(a, i)], products, i)
+            if grp == 0 and st < 2:
+                quantize_hidden(st + 2, 0, 2)
+            do_quant(a)
+            do_inter(a, "G")
+            if a in (1, 4):
+                load_wq_all(2 + a // 4)
+            add_pair(nc.vector if a in V_ADDS else nc.gpsimd, grp, products, i0)

@@ -36,12 +36,21 @@ TWO_PI_LOW = TWO_PI - TWO_PI_HIGH
 V_ADDS = (19,)
 OFFLOAD = ()
 WK_SCALAR = ((0, 1), (0, 3), (1, 1), (1, 3))
-WIDEN = ((8, 0, (0, 1)), (7, 0, (2, 3)), (7, 1, (0,)), (6, 1, (1,)), (5, 1, (2,)), (4, 1, (3,)))
-SPASS = ((5, 0), (4, 1))
-UNITS = ((5, 1, 0), (4, 1, 1), (3, 1, 2), (2, 1, 3))
-UNITS1 = ((5, 0, 0), (5, 0, 1), (4, 0, 2), (4, 0, 3), (3, 1, 0), (3, 1, 1), (2, 1, 2), (2, 1, 3))
-INTER = ((4, 0, "G"), (3, 1, "S"))
-QUANT = ((3, 0), (2, 1))
+FIRST = {
+    "widen": (),
+    "spass": (),
+    "units": ((5, ("R", 0, 0)), (5, ("R", 0, 1)), (4, ("R", 0, 2)), (4, ("R", 0, 3)), (3, ("R", 1, 0)), (3, ("R", 1, 1)), (2, ("R", 1, 2)), (2, ("R", 1, 3))),
+    "inter": (),
+    "quant": ((3, 0), (2, 1)),
+}
+LATER = {
+    "widen": ((8, 0, (0, 1)), (7, 0, (2, 3)), (7, 1, (0,)), (6, 1, (1,)), (5, 1, (2,)), (4, 1, (3,))),
+    "spass": ((5, 0), (4, 1)),
+    "units": ((5, ("R", 1, 0)), (4, ("R", 1, 1)), (3, ("R", 1, 2)), (2, ("R", 1, 3))),
+    "inter": ((4, 0, "G"), (3, 1, "S")),
+    "quant": ((3, 0), (2, 1)),
+}
+PLAN = {1: FIRST, 2: LATER, 3: LATER, 4: LATER}
 
 
 def llama3_smooth(j):
@@ -132,19 +141,17 @@ def tile_stickyllamaattention_pa_kernel(tc, hidden_states, wq_bytes, wq_scale, w
 
         freq = const.tile([P, HALF], F32, name="freq")
         nc.vector.memset(freq[:, 0:1], 1.0)
-        for m in (1, 2, 4, 8, 16, 32):
-            nc.vector.tensor_scalar(
-                out=freq[:, m : 2 * m], in0=freq[:, 0:m], scalar1=ROPE_BASE ** (-2.0 * m / D), scalar2=None, op0=ALU.mult
-            )
-        band = [j for j in range(HALF) if 0.0 < llama3_smooth(j) < 1.0]
-        for j in band:
-            nc.vector.tensor_scalar(
-                out=freq[:, j : j + 1], in0=freq[:, 0:1], scalar1=llama3_frequency(j), scalar2=None, op0=ALU.mult
-            )
-        low = band[-1] + 1
-        nc.vector.tensor_scalar(
-            out=freq[:, low:HALF], in0=freq[:, low:HALF], scalar1=1.0 / ROPE_FACTOR, scalar2=None, op0=ALU.mult
-        )
+        for n in (1, 4, 16):
+            for m in (n, 2 * n, 3 * n):
+                factor = ROPE_BASE ** (-2.0 * m / D) / (ROPE_FACTOR if m >= HALF // 2 else 1.0)
+                nc.vector.tensor_scalar(
+                    out=freq[:, m : m + n], in0=freq[:, 0:n], scalar1=factor, scalar2=None, op0=ALU.mult
+                )
+        for j in range(HALF):
+            if 0.0 < llama3_smooth(j) < 1.0:
+                nc.vector.tensor_scalar(
+                    out=freq[:, j : j + 1], in0=freq[:, 0:1], scalar1=llama3_frequency(j), scalar2=None, op0=ALU.mult
+                )
 
         angle = const.tile([P, TOKEN_TILES, HALF], F32, name="angle")
         nc.vector.tensor_tensor(
@@ -155,32 +162,25 @@ def tile_stickyllamaattention_pa_kernel(tc, hidden_states, wq_bytes, wq_scale, w
         )
         angle_flat = angle[:].rearrange("p i j -> p (i j)")
 
-        reduced = {}
-        for name, quarter in (("sin", 0.0),):
-            turns_i = const.tile([P, TOKEN_TILES * HALF], I32, name="turns_i")
-            nc.vector.tensor_scalar(
-                out=turns_i[:], in0=angle_flat, scalar1=1.0 / TWO_PI, scalar2=quarter, op0=ALU.mult, op1=ALU.add
-            )
-            turns = const.tile([P, TOKEN_TILES * HALF], F32, name="turns")
-            nc.vector.tensor_copy(out=turns[:], in_=turns_i[:])
-            part = const.tile([P, TOKEN_TILES * HALF], F32, name="part")
-            nc.vector.scalar_tensor_tensor(
-                out=part[:], in0=turns[:], scalar=-TWO_PI_HIGH, in1=angle_flat, op0=ALU.mult, op1=ALU.add
-            )
-            rest = const.tile([P, TOKEN_TILES, HALF], F32, name="rest_" + name)
-            nc.vector.scalar_tensor_tensor(
-                out=rest[:].rearrange("p i j -> p (i j)"), in0=turns[:], scalar=-TWO_PI_LOW, in1=part[:], op0=ALU.mult, op1=ALU.add
-            )
-            reduced[name] = rest
+        turns = const.tile([P, TOKEN_TILES * HALF], I32, name="turns")
+        nc.vector.tensor_scalar(out=turns[:], in0=angle_flat, scalar1=1.0 / TWO_PI, scalar2=None, op0=ALU.mult)
+        part = const.tile([P, TOKEN_TILES * HALF], F32, name="part")
+        nc.vector.scalar_tensor_tensor(
+            out=part[:], in0=turns[:], scalar=-TWO_PI_HIGH, in1=angle_flat, op0=ALU.mult, op1=ALU.add
+        )
+        rest = const.tile([P, TOKEN_TILES, HALF], F32, name="rest")
+        nc.vector.scalar_tensor_tensor(
+            out=rest[:].rearrange("p i j -> p (i j)"), in0=turns[:], scalar=-TWO_PI_LOW, in1=part[:], op0=ALU.mult, op1=ALU.add
+        )
 
         table = const.tile([P, TOKEN_TILES, 2, 2, HALF], F32, name="table")
 
-        half_sin = const.tile([P, TOKEN_TILES, HALF], F32, name="turns")
+        half_sin = const.tile([P, TOKEN_TILES, HALF], F32, name="half_sin")
         square = const.tile([P, TOKEN_TILES, HALF], F32, name="part")
 
         def fill_table():
-            nc.scalar.activation(out=half_sin[:], in_=reduced["sin"][:], func=ACT.Sin, scale=0.5)
-            nc.scalar.activation(out=table[:, :, 1, 0, :], in_=reduced["sin"][:], func=ACT.Sin)
+            nc.scalar.activation(out=half_sin[:], in_=rest[:], func=ACT.Sin, scale=0.5)
+            nc.scalar.activation(out=table[:, :, 1, 0, :], in_=rest[:], func=ACT.Sin)
             nc.gpsimd.tensor_tensor(out=square[:], in0=half_sin[:], in1=half_sin[:], op=ALU.mult)
             for half in range(2):
                 nc.gpsimd.tensor_scalar(
@@ -191,7 +191,7 @@ def tile_stickyllamaattention_pa_kernel(tc, hidden_states, wq_bytes, wq_scale, w
             )
 
         def transposes(words, pool):
-            bank = pool.tile([P, 2, 2, P], F32, name="bank")
+            bank = pool.tile([P, 2, 2, P], F32, name="acc" if pool is psum_a else "bank")
             for gg in range(2):
                 for u in range(2):
                     nc.tensor.transpose(bank[:, u, gg, :], words[:, 256 * gg + u : 256 * (gg + 1) : 2], ident[:])
@@ -247,7 +247,7 @@ def tile_stickyllamaattention_pa_kernel(tc, hidden_states, wq_bytes, wq_scale, w
         def bank_of_wk(gp, r):
             if (gp, r) == (0, 0):
                 new_group(0)
-            bank = transposes(wk_raw[(gp, r)][:].bitcast(F32), psum_v)
+            bank = transposes(wk_raw[(gp, r)][:].bitcast(F32), psum_a)
             target = as_words(w_grouped[0], N)[:, 2 * gp : 2 * gp + 2, P * r : P * (r + 1), :]
             if (gp, r) in WK_SCALAR:
                 nc.scalar.copy(out=target, in_=bank[:].rearrange("p u g n -> p g n u"))
@@ -278,19 +278,33 @@ def tile_stickyllamaattention_pa_kernel(tc, hidden_states, wq_bytes, wq_scale, w
 
         unit_banks = {}
 
-        def turn_unit(grp, gp, r):
+        def turn_unit(grp, unit):
             if grp not in w_grouped:
                 new_group(grp)
-            unit_banks[(grp, gp, r)] = transposes(wides[(grp, gp, r)][:].bitcast(F32), psum_v)
+            kind, x, y = unit
+            if kind == "R":
+                unit_banks[(grp, unit)] = transposes(wides[(grp, x, y)][:].bitcast(F32), psum_v)
+                return
+            bank = psum_v.tile([P, 2, 2, P], F32, name="bank")
+            unit_banks[(grp, unit)] = bank
+            for rr in range(2):
+                words = wides[(grp, x // 2, 2 * y + rr)][:].bitcast(F32)
+                for u in range(2):
+                    nc.tensor.transpose(bank[:, u, rr, :], words[:, 256 * (x % 2) + u : 256 * (x % 2 + 1) : 2], ident[:])
 
-        def scale_unit(grp, gp, r):
+        def scale_unit(grp, unit):
+            kind, x, y = unit
+            bank = unit_banks[(grp, unit)]
+            if kind == "R":
+                out = w_grouped[grp][:, 2 * x : 2 * x + 2, P * y : P * (y + 1), :]
+                scales = scale4[:, 2 * x : 2 * x + 2, :].unsqueeze(2).to_broadcast([P, 2, P, 4])
+            else:
+                out = w_grouped[grp][:, x, 2 * P * y : 2 * P * (y + 1), :]
+                scales = scale4[:, x, :].unsqueeze(1).to_broadcast([P, 2 * P, 4])
             nc.vector.tensor_tensor(
-                out=w_grouped[grp][:, 2 * gp : 2 * gp + 2, P * r : P * (r + 1), :],
-                in0=unit_banks[(grp, gp, r)][:]
-                .rearrange("p u g n -> p u (g n)")
-                .bitcast(BF16)
-                .rearrange("p u (m e) -> p m u e", e=2),
-                in1=scale4[:, 2 * gp : 2 * gp + 2, :].unsqueeze(2).to_broadcast([P, 2, P, 4]),
+                out=out,
+                in0=bank[:].rearrange("p u g n -> p u (g n)").bitcast(BF16).rearrange("p u (m e) -> p m u e", e=2),
+                in1=scales,
                 op=ALU.mult,
             )
 
@@ -368,7 +382,7 @@ def tile_stickyllamaattention_pa_kernel(tc, hidden_states, wq_bytes, wq_scale, w
                 op1=ALU.add,
             )
 
-        ctx.enter_context(tc.manual_schedule(engines={mybir.EngineType.DVE}))
+        ctx.enter_context(tc.manual_schedule())
         STEPS = GROUPS * TOKEN_TILES // 2
 
         def add_pair(engine, grp, products, i0):
@@ -392,53 +406,43 @@ def tile_stickyllamaattention_pa_kernel(tc, hidden_states, wq_bytes, wq_scale, w
                 for i in (2 * (b % 4), 2 * (b % 4) + 1):
                     sources[(b, i)] = project(b // 4, i)
 
-        def due(a, lead):
-            nxt, rest = divmod(a + lead, 4)
-            return nxt if rest == 0 and 1 <= nxt < GROUPS else None
+        def due(a, what):
+            found = []
+            for nxt in range(1, GROUPS):
+                for entry in PLAN[nxt][what]:
+                    if 4 * nxt - a == entry[0]:
+                        found.append((nxt,) + entry[1:])
+            return found
 
         def do_widen(a):
-            for lead, gp, rows in WIDEN:
-                nxt = due(a, lead)
-                if nxt and nxt > 1:
-                    for r in rows:
-                        widen(nxt, gp, r)
+            for nxt, gp, rows in due(a, "widen"):
+                for r in rows:
+                    widen(nxt, gp, r)
 
         def feed_units(a):
-            for nxt in range(1, GROUPS):
-                for lead, gp, r in UNITS1 if nxt == 1 else UNITS:
-                    if 4 * nxt - a == lead:
-                        turn_unit(nxt, gp, r)
-
-        def feed_passes(a):
-            for lead, g in SPASS:
-                nxt = due(a, lead)
-                if nxt and nxt > 1:
-                    turn_pass(nxt, g)
-
-        def do_passes(a):
-            for lead, g in SPASS:
-                nxt = due(a, lead)
-                if nxt and nxt > 1:
-                    scale_pass(nxt, g)
+            for nxt, unit in due(a, "units"):
+                turn_unit(nxt, unit)
 
         def do_units(a):
-            for nxt in range(1, GROUPS):
-                for lead, gp, r in UNITS1 if nxt == 1 else UNITS:
-                    if 4 * nxt - a == lead:
-                        scale_unit(nxt, gp, r)
+            for nxt, unit in due(a, "units"):
+                scale_unit(nxt, unit)
+
+        def feed_passes(a):
+            for nxt, g in due(a, "spass"):
+                turn_pass(nxt, g)
+
+        def do_passes(a):
+            for nxt, g in due(a, "spass"):
+                scale_pass(nxt, g)
 
         def do_inter(a, engine):
-            for lead, g, e in INTER:
-                nxt = due(a, lead)
-                if nxt and nxt > 1:
-                    if e == engine:
-                        interleave_pass(nxt, g, e)
+            for nxt, g, e in due(a, "inter"):
+                if e == engine:
+                    interleave_pass(nxt, g, e)
 
         def do_quant(a):
-            for lead, gp in QUANT:
-                nxt = due(a, lead)
-                if nxt:
-                    quantize_weights(nxt, gp)
+            for nxt, gp in due(a, "quant"):
+                quantize_weights(nxt, gp)
 
         turn_hidden(0)
         for r in range(GROUP_HEADS):
@@ -453,29 +457,28 @@ def tile_stickyllamaattention_pa_kernel(tc, hidden_states, wq_bytes, wq_scale, w
         for r in range(2):
             widen(1, 0, r)
         feed_units(-1)
-        project_step(0)
         turn_hidden(2)
+        project_step(0)
         turn_hidden(3)
         for r in range(2, 4):
             widen(1, 0, r)
         do_units(-1)
-        feed_units(0)
-        quantize_hidden(1, 0, 2)
         turn_hidden(4)
-        turn_hidden(5)
+        feed_units(0)
 
         for a in range(STEPS):
             grp, st = divmod(a, 4)
             i0 = 2 * st
+            first = grp == 0 and st < 3
             do_passes(a)
-            project_step(a + 1)
+            if not first:
+                project_step(a + 1)
             if a == 0:
-                turn_hidden(6)
-                turn_hidden(7)
-                for r in range(GROUP_HEADS):
+                for r in range(2):
                     widen(1, 1, r)
-            do_units(a)
-            feed_units(a + 1)
+            if not first:
+                do_units(a)
+                feed_units(a + 1)
             do_inter(a, "S")
             do_widen(a)
             feed_passes(a + 1)
@@ -488,10 +491,30 @@ def tile_stickyllamaattention_pa_kernel(tc, hidden_states, wq_bytes, wq_scale, w
             for i in (i0, i0 + 1):
                 if (grp, i) not in OFFLOAD:
                     multiply(nc.vector, sources[(a, i)], products, i)
-            if grp == 0 and st < 2:
-                quantize_hidden(st + 2, 0, 2)
+            if first:
+                quantize_hidden(st + 1, 0, 2)
+                project_step(a + 1)
+                do_units(a)
+                if st < 2:
+                    turn_hidden(5 + 2 * st)
+                feed_units(a + 1)
+                if st == 0:
+                    turn_hidden(6)
+                    for r in range(2, 4):
+                        widen(1, 1, r)
             do_quant(a)
             do_inter(a, "G")
             if a in (1, 4):
                 load_wq_all(2 + a // 4)
-            add_pair(nc.vector if a in V_ADDS else nc.gpsimd, grp, products, i0)
+            if a == STEPS - 1:
+                for n, engine in enumerate((nc.gpsimd, nc.vector)):
+                    result = resultp.tile([P, GROUP_HEADS, D], F32, name="result")
+                    engine.tensor_tensor(
+                        out=result[:].rearrange("p h (o j) -> p h o j", o=2),
+                        in0=products[:, :, n, :, 0, :],
+                        in1=products[:, :, n, :, 1, :],
+                        op=ALU.add,
+                    )
+                    nc.sync.dma_start(out=q_view[:, GROUP_HEADS * (grp - 1) : GROUP_HEADS * grp, i0 + n, :], in_=result[:])
+            else:
+                add_pair(nc.gpsimd, grp, products, i0)

@@ -33,9 +33,9 @@ TWO_PI = 2.0 * PI
 TWO_PI_HIGH = 6.28125
 TWO_PI_LOW = TWO_PI - TWO_PI_HIGH
 
-V_ADDS = (19,)
-OFFLOAD = ()
-WK_SCALAR = ((0, 1), (0, 3), (1, 1), (1, 3))
+V_ADDS = ()
+OFFLOAD = ((13, 1), (7, 0), (3, 1), (11, 1), (5, 1))
+WK_SCALAR = ((0, 0), (1, 0), (1, 2))
 FIRST = {
     "widen": (),
     "spass": (),
@@ -43,13 +43,8 @@ FIRST = {
     "inter": (),
     "quant": ((3, 0), (2, 1)),
 }
-LATER = {
-    "widen": ((8, 0, (0, 1)), (7, 0, (2, 3)), (7, 1, (0,)), (6, 1, (1,)), (5, 1, (2,)), (4, 1, (3,))),
-    "spass": ((5, 0), (4, 1)),
-    "units": ((5, ("R", 1, 0)), (4, ("R", 1, 1)), (3, ("R", 1, 2)), (2, ("R", 1, 3))),
-    "inter": ((4, 0, "G"), (3, 1, "S")),
-    "quant": ((3, 0), (2, 1)),
-}
+LATER = {'widen': ((7, 0, (0, 1, 2, 3)), (7, 1, (0,)), (6, 1, (1, 2)), (4, 1, (3,))), 'spass': ((5, 0), (4, 1)), 'units': ((5, ('R', 1, 0)), (4, ('R', 1, 1)), (3, ('R', 1, 2)), (3, ('R', 1, 3))), 'inter': ((5, 0, 'S'), (3, 1, 'S')), 'quant': ((3, 0), (2, 1))}
+ORDER = ('pass', 'interS', 'feedp', 'units', 'widen', 'feedu', 'proj', 'interG', 'rope', 'add', 'quant')
 PLAN = {1: FIRST, 2: LATER, 3: LATER, 4: LATER}
 
 
@@ -78,13 +73,13 @@ def tile_stickyllamaattention_pa_kernel(tc, hidden_states, wq_bytes, wq_scale, w
         raw = ctx.enter_context(tc.tile_pool(name="raw", bufs=1))
         xpool = ctx.enter_context(tc.tile_pool(name="xpool", bufs=8))
         wqpool = ctx.enter_context(tc.tile_pool(name="wqpool", bufs=4))
-        widep = ctx.enter_context(tc.tile_pool(name="widep", bufs=8))
+        widep = ctx.enter_context(tc.tile_pool(name="widep", bufs=10))
         planesp = ctx.enter_context(tc.tile_pool(name="planesp", bufs=2))
         groupedp = ctx.enter_context(tc.tile_pool(name="groupedp", bufs=2))
         codes = ctx.enter_context(tc.tile_pool(name="codes", bufs=1))
         wcodes = ctx.enter_context(tc.tile_pool(name="wcodes", bufs=2))
         ropep = ctx.enter_context(tc.tile_pool(name="ropep", bufs=3))
-        resultp = ctx.enter_context(tc.tile_pool(name="resultp", bufs=4))
+        resultp = ctx.enter_context(tc.tile_pool(name="resultp", bufs=3))
         stagep = ctx.enter_context(tc.tile_pool(name="stagep", bufs=1))
         psum_v = ctx.enter_context(tc.psum_pool(name="psum_v", bufs=2))
         psum_s = ctx.enter_context(tc.psum_pool(name="psum_s", bufs=2))
@@ -277,6 +272,8 @@ def tile_stickyllamaattention_pa_kernel(tc, hidden_states, wq_bytes, wq_scale, w
             )
 
         unit_banks = {}
+        done = set()
+        quantized = set()
 
         def turn_unit(grp, unit):
             if grp not in w_grouped:
@@ -295,6 +292,8 @@ def tile_stickyllamaattention_pa_kernel(tc, hidden_states, wq_bytes, wq_scale, w
         def scale_unit(grp, unit):
             kind, x, y = unit
             bank = unit_banks[(grp, unit)]
+            for q in range(2):
+                done.add((grp, 2 * x + q, y) if kind == "R" else (grp, x, 2 * y + q))
             if kind == "R":
                 out = w_grouped[grp][:, 2 * x : 2 * x + 2, P * y : P * (y + 1), :]
                 scales = scale4[:, 2 * x : 2 * x + 2, :].unsqueeze(2).to_broadcast([P, 2, P, 4])
@@ -309,6 +308,8 @@ def tile_stickyllamaattention_pa_kernel(tc, hidden_states, wq_bytes, wq_scale, w
             )
 
         def quantize_weights(grp, gp):
+            assert grp == 0 or all((grp, 2 * gp + q, r) in done for q in range(2) for r in range(4)), "stale"
+            quantized.add((grp, gp))
             passes = slice(2 * gp, 2 * gp + 2)
             nc.vector.quantize_mx(
                 out=w_codes[grp][:, passes, :].rearrange("p g n -> p (g n)").bitcast(FP8X4),
@@ -317,6 +318,7 @@ def tile_stickyllamaattention_pa_kernel(tc, hidden_states, wq_bytes, wq_scale, w
             )
 
         def project(grp, i):
+            assert (grp, 0) in quantized and (grp, 1) in quantized, "stale codes"
             acc = psum_a.tile([P, N], F32, name="acc")
             for g in range(PASSES):
                 cols = slice(P * g, P * (g + 1))
@@ -347,9 +349,9 @@ def tile_stickyllamaattention_pa_kernel(tc, hidden_states, wq_bytes, wq_scale, w
                 new_group(grp)
             for u in range(2):
                 pass_banks[(grp, g, u)] = psum_s.tile([P, GROUP_HEADS, P], F32, name="bank")
-            for r in range(GROUP_HEADS):
-                words = wides[(grp, g // 2, r)][:].bitcast(F32)
-                for u in range(2):
+            for u in range(2):
+                for r in range(GROUP_HEADS):
+                    words = wides[(grp, g // 2, r)][:].bitcast(F32)
                     nc.tensor.transpose(
                         pass_banks[(grp, g, u)][:, r, :], words[:, 256 * (g % 2) + u : 256 * (g % 2 + 1) : 2], ident[:]
                     )
@@ -370,6 +372,8 @@ def tile_stickyllamaattention_pa_kernel(tc, hidden_states, wq_bytes, wq_scale, w
                     )
 
         def interleave_pass(grp, g, engine):
+            for r in range(4):
+                done.add((grp, g, r))
             if engine == "S":
                 nc.scalar.copy(out=w_grouped[grp][:, g, :, :], in_=planes[(grp, g)][:].rearrange("p t n -> p n t"))
                 return
@@ -466,46 +470,49 @@ def tile_stickyllamaattention_pa_kernel(tc, hidden_states, wq_bytes, wq_scale, w
         turn_hidden(4)
         feed_units(0)
 
-        for a in range(STEPS):
-            grp, st = divmod(a, 4)
-            i0 = 2 * st
-            first = grp == 0 and st < 3
+        def FIRST_BODY(a):
+            st = a
             do_passes(a)
-            if not first:
-                project_step(a + 1)
             if a == 0:
                 for r in range(2):
                     widen(1, 1, r)
-            if not first:
-                do_units(a)
-                feed_units(a + 1)
             do_inter(a, "S")
             do_widen(a)
             feed_passes(a + 1)
-            products = ropep.tile([P, GROUP_HEADS, 2, 2, 2, HALF], F32, name="products")
-            for i in (i0, i0 + 1):
-                if (grp, i) in OFFLOAD:
-                    staged = stagep.tile([P, N], F32, name="staged")
-                    nc.scalar.copy(out=staged[:], in_=sources[(a, i)][:])
-                    multiply(nc.gpsimd, staged, products, i)
-            for i in (i0, i0 + 1):
-                if (grp, i) not in OFFLOAD:
-                    multiply(nc.vector, sources[(a, i)], products, i)
-            if first:
-                quantize_hidden(st + 1, 0, 2)
-                project_step(a + 1)
-                do_units(a)
-                if st < 2:
-                    turn_hidden(5 + 2 * st)
-                feed_units(a + 1)
-                if st == 0:
-                    turn_hidden(6)
-                    for r in range(2, 4):
-                        widen(1, 1, r)
+            rope(a)
+            quantize_hidden(st + 1, 0, 2)
+            project_step(a + 1)
+            do_units(a)
+            if st < 2:
+                turn_hidden(5 + 2 * st)
+            feed_units(a + 1)
+            if st == 0:
+                turn_hidden(6)
+                for r in range(2, 4):
+                    widen(1, 1, r)
             do_quant(a)
             do_inter(a, "G")
-            if a in (1, 4):
-                load_wq_all(2 + a // 4)
+            finish(a, held[a])
+
+        held = {}
+
+        def rope(a):
+            grp, st = divmod(a, 4)
+            i0 = 2 * st
+            products = ropep.tile([P, GROUP_HEADS, 2, 2, 2, HALF], F32, name="products")
+            off = [i for i in (i0, i0 + 1) if (a, i - i0) in OFFLOAD]
+            for i in off:
+                staged = stagep.tile([P, N], F32, name="staged")
+                nc.scalar.copy(out=staged[:], in_=sources[(a, i)][:])
+                multiply(nc.gpsimd, staged, products, i)
+            for i in (i0, i0 + 1):
+                if i not in off:
+                    multiply(nc.vector, sources[(a, i)], products, i)
+            held[a] = products
+
+        def finish(a, products):
+            grp, st = divmod(a, 4)
+            i0 = 2 * st
             if a == STEPS - 1:
                 for n, engine in enumerate((nc.gpsimd, nc.vector)):
                     result = resultp.tile([P, GROUP_HEADS, D], F32, name="result")
@@ -517,4 +524,28 @@ def tile_stickyllamaattention_pa_kernel(tc, hidden_states, wq_bytes, wq_scale, w
                     )
                     nc.sync.dma_start(out=q_view[:, GROUP_HEADS * (grp - 1) : GROUP_HEADS * grp, i0 + n, :], in_=result[:])
             else:
-                add_pair(nc.gpsimd, grp, products, i0)
+                add_pair(nc.vector if a in V_ADDS else nc.gpsimd, grp, products, i0)
+
+        actions = {
+            "proj": lambda a: project_step(a + 1),
+            "units": lambda a: do_units(a),
+            "feedu": lambda a: feed_units(a + 1),
+            "feedp": lambda a: feed_passes(a + 1),
+            "pass": lambda a: do_passes(a),
+            "interS": lambda a: do_inter(a, "S"),
+            "interG": lambda a: do_inter(a, "G"),
+            "widen": lambda a: do_widen(a),
+            "rope": lambda a: rope(a),
+            "quant": lambda a: do_quant(a),
+            "add": lambda a: finish(a, held[a]),
+        }
+        for a in range(STEPS):
+            grp, st = divmod(a, 4)
+            i0 = 2 * st
+            if a < 3:
+                FIRST_BODY(a)
+            else:
+                for what in ORDER:
+                    actions[what](a)
+            if a in (1, 4):
+                load_wq_all(2 + a // 4)

@@ -27,25 +27,13 @@ HALF = D // 2
 GROUP_HEADS = 4
 GROUPS = (Q_HEADS + KV_HEADS) // GROUP_HEADS
 N = GROUP_HEADS * D
+GROUP_STEPS = TOKEN_TILES // 2
+STEPS = GROUPS * GROUP_STEPS
 
 PI = 3.141592653589793
 TWO_PI = 2.0 * PI
 TWO_PI_HIGH = 6.28125
 TWO_PI_LOW = TWO_PI - TWO_PI_HIGH
-
-V_ADDS = ()
-OFFLOAD = ((13, 1), (7, 0), (3, 1), (11, 1), (5, 1))
-WK_SCALAR = ((0, 0), (1, 0), (1, 2))
-FIRST = {
-    "widen": (),
-    "spass": (),
-    "units": ((5, ("R", 0, 0)), (5, ("R", 0, 1)), (4, ("R", 0, 2)), (4, ("R", 0, 3)), (3, ("R", 1, 0)), (3, ("R", 1, 1)), (2, ("R", 1, 2)), (2, ("R", 1, 3))),
-    "inter": (),
-    "quant": ((3, 0), (2, 1)),
-}
-LATER = {'widen': ((7, 0, (0, 1, 2, 3)), (7, 1, (0,)), (6, 1, (1, 2)), (4, 1, (3,))), 'spass': ((5, 0), (4, 1)), 'units': ((5, ('R', 1, 0)), (4, ('R', 1, 1)), (3, ('R', 1, 2)), (3, ('R', 1, 3))), 'inter': ((5, 0, 'S'), (3, 1, 'S')), 'quant': ((3, 0), (2, 1))}
-ORDER = ('pass', 'interS', 'feedp', 'units', 'widen', 'feedu', 'proj', 'interG', 'rope', 'add', 'quant')
-PLAN = {1: FIRST, 2: LATER, 3: LATER, 4: LATER}
 
 
 def llama3_smooth(j):
@@ -70,7 +58,7 @@ def tile_stickyllamaattention_pa_kernel(tc, hidden_states, wq_bytes, wq_scale, w
 
     with ExitStack() as ctx:
         const = ctx.enter_context(tc.tile_pool(name="const", bufs=1))
-        raw = ctx.enter_context(tc.tile_pool(name="raw", bufs=1))
+        wkpool = ctx.enter_context(tc.tile_pool(name="wkpool", bufs=1))
         xpool = ctx.enter_context(tc.tile_pool(name="xpool", bufs=8))
         wqpool = ctx.enter_context(tc.tile_pool(name="wqpool", bufs=4))
         widep = ctx.enter_context(tc.tile_pool(name="widep", bufs=10))
@@ -91,40 +79,36 @@ def tile_stickyllamaattention_pa_kernel(tc, hidden_states, wq_bytes, wq_scale, w
 
         scale4 = const.tile([P, PASSES, 4], F32, name="scale4")
         nc.scalar.dma_start(out=scale4[:], in_=wq_scale.rearrange("o (g p t) -> p (o g) t", p=P, t=4))
-        wq_raw = {}
-
-        def load_wq_all(c):
-            for gp in range(2):
-                load_wq(c, gp)
-
-        def load_wq(c, gp):
-            wq_raw[(c, gp)] = wqpool.tile([P, GROUP_HEADS, H // 2], U8, name="wq_raw")
-            nc.sync.dma_start(out=wq_raw[(c, gp)][:], in_=wq_halves[c][gp])
         wk_raw = {}
-        for gp in range(2):
-            for r in range(GROUP_HEADS):
-                wk_raw[(gp, r)] = raw.tile([P, H // 2], BF16, name="wk_raw%d_%d" % (gp, r))
+        wq_raw = {}
         x_raw = {}
+
+        def load_wk(gp):
+            for r in range(GROUP_HEADS):
+                wk_raw[(gp, r)] = wkpool.tile([P, H // 2], BF16, name="wk_raw%d_%d" % (gp, r))
+                nc.sync.dma_start(out=wk_raw[(gp, r)][:], in_=wk_rows[r][:, 1024 * gp : 1024 * (gp + 1)])
+
+        def load_wq(grp, gp):
+            wq_raw[(grp, gp)] = wqpool.tile([P, GROUP_HEADS, H // 2], U8, name="wq_raw")
+            nc.sync.dma_start(out=wq_raw[(grp, gp)][:], in_=wq_halves[grp - 1][gp])
 
         def load_hidden(i):
             x_raw[i] = xpool.tile([P, H], BF16, name="x_raw")
             nc.sync.dma_start(out=x_raw[i][:], in_=hidden_tiles[i])
 
-        def load_wk(gp):
-            for r in range(GROUP_HEADS):
-                nc.sync.dma_start(out=wk_raw[(gp, r)][:], in_=wk_rows[r][:, 1024 * gp : 1024 * (gp + 1)])
-
-        load_hidden(0)
         load_wk(0)
+        load_hidden(0)
         load_hidden(1)
-        load_wk(1)
-        load_wq(0, 0)
         load_hidden(2)
+        load_wq(1, 0)
+        load_wk(1)
         load_hidden(3)
-        load_wq(0, 1)
-        for i in range(4, TOKEN_TILES):
+        load_hidden(4)
+        load_wq(1, 1)
+        for i in range(5, TOKEN_TILES):
             load_hidden(i)
-        load_wq_all(1)
+        load_wq(2, 0)
+        load_wq(2, 1)
 
         ident = const.tile([P, P], F32, name="ident")
         make_identity(nc, ident[:])
@@ -156,7 +140,6 @@ def tile_stickyllamaattention_pa_kernel(tc, hidden_states, wq_bytes, wq_scale, w
             op=ALU.mult,
         )
         angle_flat = angle[:].rearrange("p i j -> p (i j)")
-
         turns = const.tile([P, TOKEN_TILES * HALF], I32, name="turns")
         nc.vector.tensor_scalar(out=turns[:], in0=angle_flat, scalar1=1.0 / TWO_PI, scalar2=None, op0=ALU.mult)
         part = const.tile([P, TOKEN_TILES * HALF], F32, name="part")
@@ -169,7 +152,6 @@ def tile_stickyllamaattention_pa_kernel(tc, hidden_states, wq_bytes, wq_scale, w
         )
 
         table = const.tile([P, TOKEN_TILES, 2, 2, HALF], F32, name="table")
-
         half_sin = const.tile([P, TOKEN_TILES, HALF], F32, name="half_sin")
         square = const.tile([P, TOKEN_TILES, HALF], F32, name="part")
 
@@ -185,20 +167,12 @@ def tile_stickyllamaattention_pa_kernel(tc, hidden_states, wq_bytes, wq_scale, w
                 out=table[:, :, 0, 1, :], in0=table[:, :, 1, 0, :], scalar1=-1.0, scalar2=0.0, op0=ALU.mult, op1=ALU.add
             )
 
-        def transposes(words, pool):
-            bank = pool.tile([P, 2, 2, P], F32, name="acc" if pool is psum_a else "bank")
+        def transposes(words, pool, name):
+            bank = pool.tile([P, 2, 2, P], F32, name=name)
             for gg in range(2):
                 for u in range(2):
                     nc.tensor.transpose(bank[:, u, gg, :], words[:, 256 * gg + u : 256 * (gg + 1) : 2], ident[:])
             return bank
-
-        def as_words(grouped, width):
-            return (
-                grouped[:]
-                .rearrange("p g n t -> p (g n t)")
-                .bitcast(F32)
-                .rearrange("p (g n u) -> p g n u", g=PASSES, n=width)
-            )
 
         x_codes = {}
         x_scales = {}
@@ -215,101 +189,44 @@ def tile_stickyllamaattention_pa_kernel(tc, hidden_states, wq_bytes, wq_scale, w
                 .rearrange("p (g n u) -> p g n u", g=PASSES, u=2)
             )
             for gp in range(2):
-                bank = transposes(x_raw[i][:, 1024 * gp : 1024 * (gp + 1)].bitcast(F32), psum_s)
+                bank = transposes(x_raw[i][:, 1024 * gp : 1024 * (gp + 1)].bitcast(F32), psum_s, "bank_s")
                 nc.scalar.copy(out=words[:, 2 * gp : 2 * gp + 2, :, :], in_=bank[:].rearrange("p u g n -> p g n u"))
 
-        def quantize_hidden(pair, first, count):
-            if pair not in x_codes:
-                x_codes[pair] = codes.tile([P, 2, PASSES * P], U32, name="x_codes%d" % pair, align_bytes=64)
-                x_scales[pair] = codes.tile([P, 2, PASSES * P], U8, name="x_scales%d" % pair, align_bytes=64)
-            tiles = slice(first, first + count)
+        def quantize_hidden(pair):
+            x_codes[pair] = codes.tile([P, 2, PASSES * P], U32, name="x_codes%d" % pair, align_bytes=64)
+            x_scales[pair] = codes.tile([P, 2, PASSES * P], U8, name="x_scales%d" % pair, align_bytes=64)
             nc.vector.quantize_mx(
-                out=x_codes[pair][:, tiles, :].rearrange("p i c -> p (i c)").bitcast(FP8X4),
-                scales=x_scales[pair][:, tiles, :].rearrange("p i c -> p (i c)"),
-                in_=x_grouped[pair][:, tiles, :, :, :].rearrange("p i g n t -> p (i g n t)"),
+                out=x_codes[pair][:].rearrange("p i c -> p (i c)").bitcast(FP8X4),
+                scales=x_scales[pair][:].rearrange("p i c -> p (i c)"),
+                in_=x_grouped[pair][:].rearrange("p i g n t -> p (i g n t)"),
             )
 
         w_grouped = {}
         w_codes = {}
         w_scales = {}
-        wides = {}
 
-        def new_group(grp):
-            w_grouped[grp] = groupedp.tile([P, PASSES, N, 4], BF16, name="w_grouped", align_bytes=64)
-            w_codes[grp] = wcodes.tile([P, PASSES, N], U32, name="w_codes", align_bytes=64)
-            w_scales[grp] = wcodes.tile([P, PASSES, N], U8, name="w_scales", align_bytes=64)
+        def grouped(grp):
+            if grp not in w_grouped:
+                w_grouped[grp] = groupedp.tile([P, PASSES, N, 4], BF16, name="w_grouped", align_bytes=64)
+                w_codes[grp] = wcodes.tile([P, PASSES, N], U32, name="w_codes", align_bytes=64)
+                w_scales[grp] = wcodes.tile([P, PASSES, N], U8, name="w_scales", align_bytes=64)
+            return w_grouped[grp]
 
-        def bank_of_wk(gp, r):
-            if (gp, r) == (0, 0):
-                new_group(0)
-            bank = transposes(wk_raw[(gp, r)][:].bitcast(F32), psum_a)
-            target = as_words(w_grouped[0], N)[:, 2 * gp : 2 * gp + 2, P * r : P * (r + 1), :]
-            if (gp, r) in WK_SCALAR:
+        def turn_wk(gp, r):
+            bank = transposes(wk_raw[(gp, r)][:].bitcast(F32), psum_a, "acc")
+            words = (
+                grouped(0)[:]
+                .rearrange("p g n t -> p (g n t)")
+                .bitcast(F32)
+                .rearrange("p (g n u) -> p g n u", g=PASSES, n=N)
+            )
+            target = words[:, 2 * gp : 2 * gp + 2, P * r : P * (r + 1), :]
+            if gp == 1 and r > 0 or gp == 0 and r % 2 == 1:
                 nc.scalar.copy(out=target, in_=bank[:].rearrange("p u g n -> p g n u"))
             else:
                 nc.vector.tensor_copy(out=target, in_=bank[:].rearrange("p u g n -> p g n u"))
 
-        def widen(grp, gp, r):
-            wides[(grp, gp, r)] = widep.tile([P, 1024], BF16, name="wide")
-            nc.scalar.copy(
-                out=wides[(grp, gp, r)][:], in_=wq_raw[(grp - 1, gp)][:, r, :].bitcast(FP8)
-            )
-
-        banks = {}
-
-        def turn_wq(grp, gp, r):
-            banks[(grp, gp, r)] = transposes(wides[(grp, gp, r)][:].bitcast(F32), psum_v)
-
-        def scale_wq(grp, gp, r):
-            nc.vector.tensor_tensor(
-                out=w_grouped[grp][:, 2 * gp : 2 * gp + 2, P * r : P * (r + 1), :],
-                in0=banks[(grp, gp, r)][:]
-                .rearrange("p u g n -> p u (g n)")
-                .bitcast(BF16)
-                .rearrange("p u (m e) -> p m u e", e=2),
-                in1=scale4[:, 2 * gp : 2 * gp + 2, :].unsqueeze(2).to_broadcast([P, 2, P, 4]),
-                op=ALU.mult,
-            )
-
-        unit_banks = {}
-        done = set()
-        quantized = set()
-
-        def turn_unit(grp, unit):
-            if grp not in w_grouped:
-                new_group(grp)
-            kind, x, y = unit
-            if kind == "R":
-                unit_banks[(grp, unit)] = transposes(wides[(grp, x, y)][:].bitcast(F32), psum_v)
-                return
-            bank = psum_v.tile([P, 2, 2, P], F32, name="bank")
-            unit_banks[(grp, unit)] = bank
-            for rr in range(2):
-                words = wides[(grp, x // 2, 2 * y + rr)][:].bitcast(F32)
-                for u in range(2):
-                    nc.tensor.transpose(bank[:, u, rr, :], words[:, 256 * (x % 2) + u : 256 * (x % 2 + 1) : 2], ident[:])
-
-        def scale_unit(grp, unit):
-            kind, x, y = unit
-            bank = unit_banks[(grp, unit)]
-            for q in range(2):
-                done.add((grp, 2 * x + q, y) if kind == "R" else (grp, x, 2 * y + q))
-            if kind == "R":
-                out = w_grouped[grp][:, 2 * x : 2 * x + 2, P * y : P * (y + 1), :]
-                scales = scale4[:, 2 * x : 2 * x + 2, :].unsqueeze(2).to_broadcast([P, 2, P, 4])
-            else:
-                out = w_grouped[grp][:, x, 2 * P * y : 2 * P * (y + 1), :]
-                scales = scale4[:, x, :].unsqueeze(1).to_broadcast([P, 2 * P, 4])
-            nc.vector.tensor_tensor(
-                out=out,
-                in0=bank[:].rearrange("p u g n -> p u (g n)").bitcast(BF16).rearrange("p u (m e) -> p m u e", e=2),
-                in1=scales,
-                op=ALU.mult,
-            )
-
         def quantize_weights(grp, gp):
-            assert grp == 0 or all((grp, 2 * gp + q, r) in done for q in range(2) for r in range(4)), "stale"
-            quantized.add((grp, gp))
             passes = slice(2 * gp, 2 * gp + 2)
             nc.vector.quantize_mx(
                 out=w_codes[grp][:, passes, :].rearrange("p g n -> p (g n)").bitcast(FP8X4),
@@ -317,38 +234,37 @@ def tile_stickyllamaattention_pa_kernel(tc, hidden_states, wq_bytes, wq_scale, w
                 in_=w_grouped[grp][:, passes, :, :].rearrange("p g n t -> p (g n t)"),
             )
 
-        def project(grp, i):
-            assert (grp, 0) in quantized and (grp, 1) in quantized, "stale codes"
-            acc = psum_a.tile([P, N], F32, name="acc")
-            for g in range(PASSES):
-                cols = slice(P * g, P * (g + 1))
-                nc.tensor.matmul_mx(
-                    out=acc[:],
-                    lhsT=x_codes[i // 2][:, i % 2, cols].bitcast(FP8X4),
-                    lhsT_scale=x_scales[i // 2][:, i % 2, cols],
-                    rhs=w_codes[grp][:, g, :].bitcast(FP8X4),
-                    rhs_scale=w_scales[grp][:, g, :],
-                    start=(g == 0),
-                    stop=(g == PASSES - 1),
-                )
-            return acc
+        wides = {}
 
-        def multiply(engine, source, products, i):
-            engine.tensor_tensor(
-                out=products[:, :, i % 2, :, :, :].rearrange("p h o s j -> p h o (s j)"),
-                in0=source[:].rearrange("p (h d) -> p h d", h=GROUP_HEADS).unsqueeze(2).to_broadcast([P, GROUP_HEADS, 2, D]),
-                in1=table[:, i, :, :, :].rearrange("p o s j -> p o (s j)").unsqueeze(1).to_broadcast([P, GROUP_HEADS, 2, D]),
-                op=ALU.mult,
-            )
+        def widen(grp, gp, rows):
+            for r in rows:
+                wides[(grp, gp, r)] = widep.tile([P, 1024], BF16, name="wide")
+                nc.scalar.copy(out=wides[(grp, gp, r)][:], in_=wq_raw[(grp, gp)][:, r, :].bitcast(FP8))
+
+        unit_banks = {}
+
+        def turn_units(grp, gp, rows):
+            for r in rows:
+                unit_banks[(grp, gp, r)] = transposes(wides[(grp, gp, r)][:].bitcast(F32), psum_v, "bank_v")
+
+        def scale_units(grp, gp, rows):
+            for r in rows:
+                nc.vector.tensor_tensor(
+                    out=grouped(grp)[:, 2 * gp : 2 * gp + 2, P * r : P * (r + 1), :],
+                    in0=unit_banks[(grp, gp, r)][:]
+                    .rearrange("p u g n -> p u (g n)")
+                    .bitcast(BF16)
+                    .rearrange("p u (m e) -> p m u e", e=2),
+                    in1=scale4[:, 2 * gp : 2 * gp + 2, :].unsqueeze(2).to_broadcast([P, 2, P, 4]),
+                    op=ALU.mult,
+                )
 
         pass_banks = {}
         planes = {}
 
         def turn_pass(grp, g):
-            if grp not in w_grouped:
-                new_group(grp)
             for u in range(2):
-                pass_banks[(grp, g, u)] = psum_s.tile([P, GROUP_HEADS, P], F32, name="bank")
+                pass_banks[(grp, g, u)] = psum_s.tile([P, GROUP_HEADS, P], F32, name="bank_s")
             for u in range(2):
                 for r in range(GROUP_HEADS):
                     words = wides[(grp, g // 2, r)][:].bitcast(F32)
@@ -371,181 +287,171 @@ def tile_stickyllamaattention_pa_kernel(tc, hidden_states, wq_bytes, wq_scale, w
                         out=planes[(grp, g)][:, t, :], in_=pairs[:, :, e], func=ACT.Copy, scale=scale4[:, g, t : t + 1]
                     )
 
-        def interleave_pass(grp, g, engine):
-            for r in range(4):
-                done.add((grp, g, r))
-            if engine == "S":
-                nc.scalar.copy(out=w_grouped[grp][:, g, :, :], in_=planes[(grp, g)][:].rearrange("p t n -> p n t"))
-                return
-            nc.gpsimd.tensor_scalar(
-                out=w_grouped[grp][:, g, :, :],
-                in0=planes[(grp, g)][:].rearrange("p t n -> p n t"),
-                scalar1=1.0,
-                scalar2=0.0,
-                op0=ALU.mult,
-                op1=ALU.add,
+        def interleave_pass(grp, g):
+            nc.scalar.copy(out=grouped(grp)[:, g, :, :], in_=planes[(grp, g)][:].rearrange("p t n -> p n t"))
+
+        accs = {}
+
+        def project(step):
+            grp, pair = divmod(step, GROUP_STEPS)
+            for n in range(2):
+                acc = psum_a.tile([P, N], F32, name="acc")
+                accs[(step, n)] = acc
+                for g in range(PASSES):
+                    cols = slice(P * g, P * (g + 1))
+                    nc.tensor.matmul_mx(
+                        out=acc[:],
+                        lhsT=x_codes[pair][:, n, cols].bitcast(FP8X4),
+                        lhsT_scale=x_scales[pair][:, n, cols],
+                        rhs=w_codes[grp][:, g, :].bitcast(FP8X4),
+                        rhs_scale=w_scales[grp][:, g, :],
+                        start=(g == 0),
+                        stop=(g == PASSES - 1),
+                    )
+
+        products = {}
+
+        def multiply(engine, source, step, n):
+            i = 2 * (step % GROUP_STEPS) + n
+            engine.tensor_tensor(
+                out=products[step][:, :, n, :, :, :].rearrange("p h o s j -> p h o (s j)"),
+                in0=source[:].rearrange("p (h d) -> p h d", h=GROUP_HEADS).unsqueeze(2).to_broadcast([P, GROUP_HEADS, 2, D]),
+                in1=table[:, i, :, :, :].rearrange("p o s j -> p o (s j)").unsqueeze(1).to_broadcast([P, GROUP_HEADS, 2, D]),
+                op=ALU.mult,
             )
+
+        def rope_products(step):
+            products[step] = ropep.tile([P, GROUP_HEADS, 2, 2, 2, HALF], F32, name="products")
+            shared = step % GROUP_STEPS == 0 and step < STEPS - GROUP_STEPS
+            if shared:
+                staged = stagep.tile([P, N], F32, name="staged")
+                nc.scalar.copy(out=staged[:], in_=accs[(step, 1)][:])
+                multiply(nc.gpsimd, staged, step, 1)
+            multiply(nc.vector, accs[(step, 0)], step, 0)
+            if not shared:
+                multiply(nc.vector, accs[(step, 1)], step, 1)
+
+        def rope_sum(step):
+            grp, pair = divmod(step, GROUP_STEPS)
+            view = k_view if grp == 0 else q_view[:, GROUP_HEADS * (grp - 1) : GROUP_HEADS * grp, :, :]
+            if step < STEPS - 1:
+                result = resultp.tile([P, GROUP_HEADS, 2, D], F32, name="result")
+                nc.gpsimd.tensor_tensor(
+                    out=result[:].rearrange("p h i (o j) -> p (h i o) j", o=2),
+                    in0=products[step][:, :, :, :, 0, :].rearrange("p h i o j -> p (h i o) j"),
+                    in1=products[step][:, :, :, :, 1, :].rearrange("p h i o j -> p (h i o) j"),
+                    op=ALU.add,
+                )
+                nc.sync.dma_start(out=view[:, :, 2 * pair : 2 * pair + 2, :], in_=result[:])
+                return
+            for n, engine in enumerate((nc.gpsimd, nc.vector)):
+                result = resultp.tile([P, GROUP_HEADS, D], F32, name="result")
+                engine.tensor_tensor(
+                    out=result[:].rearrange("p h (o j) -> p h o j", o=2),
+                    in0=products[step][:, :, n, :, 0, :],
+                    in1=products[step][:, :, n, :, 1, :],
+                    op=ALU.add,
+                )
+                nc.sync.dma_start(out=view[:, :, 2 * pair + n, :], in_=result[:])
 
         ctx.enter_context(tc.manual_schedule())
-        STEPS = GROUPS * TOKEN_TILES // 2
+        first, last = (0, 1), (2, 3)
+        every = first + last
 
-        def add_pair(engine, grp, products, i0):
-            result = resultp.tile([P, GROUP_HEADS, 2, D], F32, name="result")
-            engine.tensor_tensor(
-                out=result[:].rearrange("p h i (o j) -> p (h i o) j", o=2),
-                in0=products[:, :, :, :, 0, :].rearrange("p h i o j -> p (h i o) j"),
-                in1=products[:, :, :, :, 1, :].rearrange("p h i o j -> p (h i o) j"),
-                op=ALU.add,
-            )
-            if grp == 0:
-                target = k_view[:, :, i0 : i0 + 2, :]
-            else:
-                target = q_view[:, GROUP_HEADS * (grp - 1) : GROUP_HEADS * grp, i0 : i0 + 2, :]
-            nc.sync.dma_start(out=target, in_=result[:])
-
-        sources = {}
-
-        def project_step(b):
-            if b < STEPS:
-                for i in (2 * (b % 4), 2 * (b % 4) + 1):
-                    sources[(b, i)] = project(b // 4, i)
-
-        def due(a, what):
-            found = []
-            for nxt in range(1, GROUPS):
-                for entry in PLAN[nxt][what]:
-                    if 4 * nxt - a == entry[0]:
-                        found.append((nxt,) + entry[1:])
-            return found
-
-        def do_widen(a):
-            for nxt, gp, rows in due(a, "widen"):
-                for r in rows:
-                    widen(nxt, gp, r)
-
-        def feed_units(a):
-            for nxt, unit in due(a, "units"):
-                turn_unit(nxt, unit)
-
-        def do_units(a):
-            for nxt, unit in due(a, "units"):
-                scale_unit(nxt, unit)
-
-        def feed_passes(a):
-            for nxt, g in due(a, "spass"):
-                turn_pass(nxt, g)
-
-        def do_passes(a):
-            for nxt, g in due(a, "spass"):
-                scale_pass(nxt, g)
-
-        def do_inter(a, engine):
-            for nxt, g, e in due(a, "inter"):
-                if e == engine:
-                    interleave_pass(nxt, g, e)
-
-        def do_quant(a):
-            for nxt, gp in due(a, "quant"):
-                quantize_weights(nxt, gp)
-
-        turn_hidden(0)
-        for r in range(GROUP_HEADS):
-            bank_of_wk(0, r)
-        fill_table()
-        turn_hidden(1)
+        for r in every:
+            turn_wk(0, r)
+        for i in range(3):
+            turn_hidden(i)
+        widen(1, 0, first)
+        for r in every:
+            turn_wk(1, r)
+        quantize_hidden(0)
         quantize_weights(0, 0)
-        for r in range(GROUP_HEADS):
-            bank_of_wk(1, r)
-        quantize_hidden(0, 0, 2)
+        fill_table()
+        widen(1, 0, last)
+        turn_units(1, 0, first)
         quantize_weights(0, 1)
-        for r in range(2):
-            widen(1, 0, r)
-        feed_units(-1)
-        turn_hidden(2)
-        project_step(0)
         turn_hidden(3)
-        for r in range(2, 4):
-            widen(1, 0, r)
-        do_units(-1)
+        scale_units(1, 0, first)
+        project(0)
+        turn_units(1, 0, last)
         turn_hidden(4)
-        feed_units(0)
 
-        def FIRST_BODY(a):
-            st = a
-            do_passes(a)
-            if a == 0:
-                for r in range(2):
-                    widen(1, 1, r)
-            do_inter(a, "S")
-            do_widen(a)
-            feed_passes(a + 1)
-            rope(a)
-            quantize_hidden(st + 1, 0, 2)
-            project_step(a + 1)
-            do_units(a)
-            if st < 2:
-                turn_hidden(5 + 2 * st)
-            feed_units(a + 1)
-            if st == 0:
-                turn_hidden(6)
-                for r in range(2, 4):
-                    widen(1, 1, r)
-            do_quant(a)
-            do_inter(a, "G")
-            finish(a, held[a])
+        turn_hidden(5)
+        quantize_hidden(1)
+        scale_units(1, 0, last)
+        project(1)
+        quantize_weights(1, 0)
+        widen(1, 1, first)
+        rope_products(0)
+        turn_units(1, 1, first)
+        widen(1, 1, last)
+        turn_hidden(6)
+        rope_sum(0)
 
-        held = {}
+        rope_products(1)
+        quantize_hidden(2)
+        scale_units(1, 1, first)
+        turn_hidden(7)
+        widen(2, 0, every)
+        project(2)
+        rope_sum(1)
+        turn_units(1, 1, last)
+        turn_pass(2, 0)
+        load_wq(3, 0)
+        load_wq(3, 1)
 
-        def rope(a):
-            grp, st = divmod(a, 4)
-            i0 = 2 * st
-            products = ropep.tile([P, GROUP_HEADS, 2, 2, 2, HALF], F32, name="products")
-            off = [i for i in (i0, i0 + 1) if (a, i - i0) in OFFLOAD]
-            for i in off:
-                staged = stagep.tile([P, N], F32, name="staged")
-                nc.scalar.copy(out=staged[:], in_=sources[(a, i)][:])
-                multiply(nc.gpsimd, staged, products, i)
-            for i in (i0, i0 + 1):
-                if i not in off:
-                    multiply(nc.vector, sources[(a, i)], products, i)
-            held[a] = products
+        quantize_hidden(3)
+        widen(2, 1, every)
+        scale_pass(2, 0)
+        project(3)
+        rope_products(2)
+        scale_units(1, 1, last)
+        rope_sum(2)
 
-        def finish(a, products):
-            grp, st = divmod(a, 4)
-            i0 = 2 * st
-            if a == STEPS - 1:
-                for n, engine in enumerate((nc.gpsimd, nc.vector)):
-                    result = resultp.tile([P, GROUP_HEADS, D], F32, name="result")
-                    engine.tensor_tensor(
-                        out=result[:].rearrange("p h (o j) -> p h o j", o=2),
-                        in0=products[:, :, n, :, 0, :],
-                        in1=products[:, :, n, :, 1, :],
-                        op=ALU.add,
-                    )
-                    nc.sync.dma_start(out=q_view[:, GROUP_HEADS * (grp - 1) : GROUP_HEADS * grp, i0 + n, :], in_=result[:])
-            else:
-                add_pair(nc.vector if a in V_ADDS else nc.gpsimd, grp, products, i0)
-
-        actions = {
-            "proj": lambda a: project_step(a + 1),
-            "units": lambda a: do_units(a),
-            "feedu": lambda a: feed_units(a + 1),
-            "feedp": lambda a: feed_passes(a + 1),
-            "pass": lambda a: do_passes(a),
-            "interS": lambda a: do_inter(a, "S"),
-            "interG": lambda a: do_inter(a, "G"),
-            "widen": lambda a: do_widen(a),
-            "rope": lambda a: rope(a),
-            "quant": lambda a: do_quant(a),
-            "add": lambda a: finish(a, held[a]),
-        }
-        for a in range(STEPS):
-            grp, st = divmod(a, 4)
-            i0 = 2 * st
-            if a < 3:
-                FIRST_BODY(a)
-            else:
-                for what in ORDER:
-                    actions[what](a)
-            if a in (1, 4):
-                load_wq_all(2 + a // 4)
+        for step in range(3, STEPS):
+            phase = step % GROUP_STEPS
+            near = step // GROUP_STEPS + 1
+            far = near + 1
+            if near < GROUPS:
+                if phase == 0:
+                    scale_units(near, 1, first)
+                if phase == 1:
+                    scale_units(near, 1, last)
+            if far < GROUPS:
+                if phase == 1:
+                    widen(far, 0, every)
+                if phase == 2:
+                    widen(far, 1, every)
+                if phase == 3:
+                    interleave_pass(far, 0)
+                if phase == 2:
+                    scale_pass(far, 0)
+            if near < GROUPS:
+                if phase == 0:
+                    scale_pass(near, 1)
+                if phase == 1:
+                    interleave_pass(near, 1)
+                if phase == 0:
+                    turn_units(near, 1, last)
+            if far < GROUPS and phase == 3:
+                turn_units(far, 1, first)
+            rope_products(step)
+            if phase == 3 and near == 1:
+                quantize_weights(1, 1)
+            if near < GROUPS:
+                if phase == 1:
+                    quantize_weights(near, 0)
+                if phase == 2:
+                    quantize_weights(near, 1)
+            rope_sum(step)
+            if far < GROUPS:
+                if phase == 1:
+                    turn_pass(far, 0)
+                if phase == 3:
+                    turn_pass(far, 1)
+            if step == 4:
+                load_wq(4, 0)
+                load_wq(4, 1)
+            if step + 1 < STEPS:
+                project(step + 1)

@@ -288,7 +288,10 @@ def tile_stickyllamaattention_pa_kernel(tc, hidden_states, wq_bytes, wq_scale, w
                     )
 
         def interleave_pass(grp, g):
-            nc.scalar.copy(out=grouped(grp)[:, g, :, :], in_=planes[(grp, g)][:].rearrange("p t n -> p n t"))
+            nc.scalar.copy(
+                out=grouped(grp)[:, g, :, :].rearrange("p (c i) t -> p c t i", i=4),
+                in_=planes[(grp, g)][:].rearrange("p t (c i) -> p c t i", i=4),
+            )
 
         accs = {}
 
@@ -344,8 +347,8 @@ def tile_stickyllamaattention_pa_kernel(tc, hidden_states, wq_bytes, wq_scale, w
                 )
                 nc.sync.dma_start(out=view[:, :, 2 * pair : 2 * pair + 2, :], in_=result[:])
                 return
-            for n, engine in enumerate((nc.gpsimd, nc.vector)):
-                result = resultp.tile([P, GROUP_HEADS, D], F32, name="result")
+            for n, engine in enumerate((nc.vector, nc.vector)):
+                result = widep.tile([P, GROUP_HEADS, D], F32, name="wide")
                 engine.tensor_tensor(
                     out=result[:].rearrange("p h (o j) -> p h o j", o=2),
                     in0=products[step][:, :, n, :, 0, :],

@@ -26,6 +26,7 @@ TOKEN_TILES = S // P
 HALF = D // 2
 GROUP_HEADS = 4
 GROUPS = (Q_HEADS + KV_HEADS) // GROUP_HEADS
+ORDER = (1, 0, 2, 3, 4)
 N = GROUP_HEADS * D
 GROUP_STEPS = TOKEN_TILES // 2
 STEPS = GROUPS * GROUP_STEPS
@@ -70,8 +71,8 @@ def tile_stickyllamaattention_pa_kernel(tc, hidden_states, wq_bytes, wq_scale, w
         resultp = ctx.enter_context(tc.tile_pool(name="resultp", bufs=3))
         stagep = ctx.enter_context(tc.tile_pool(name="stagep", bufs=1))
         psum_v = ctx.enter_context(tc.psum_pool(name="psum_v", bufs=2))
-        psum_s = ctx.enter_context(tc.psum_pool(name="psum_s", bufs=2))
-        psum_a = ctx.enter_context(tc.psum_pool(name="psum_a", bufs=4))
+        psum_s = ctx.enter_context(tc.psum_pool(name="psum_s", bufs=3))
+        psum_a = ctx.enter_context(tc.psum_pool(name="psum_a", bufs=3))
 
         warm = const.tile([P, 2], F32, name="warm")
         nc.vector.memset(warm[:, 0:1], 0.0)
@@ -96,16 +97,15 @@ def tile_stickyllamaattention_pa_kernel(tc, hidden_states, wq_bytes, wq_scale, w
             x_raw[i] = xpool.tile([P, H], BF16, name="x_raw")
             nc.sync.dma_start(out=x_raw[i][:], in_=hidden_tiles[i])
 
-        load_wk(0)
+        load_wq(1, 0)
         load_hidden(0)
+        load_wk(0)
         load_hidden(1)
         load_hidden(2)
-        load_wq(1, 0)
-        load_wk(1)
-        load_hidden(3)
-        load_hidden(4)
         load_wq(1, 1)
-        for i in range(5, TOKEN_TILES):
+        load_hidden(3)
+        load_wk(1)
+        for i in range(4, TOKEN_TILES):
             load_hidden(i)
         load_wq(2, 0)
         load_wq(2, 1)
@@ -213,7 +213,10 @@ def tile_stickyllamaattention_pa_kernel(tc, hidden_states, wq_bytes, wq_scale, w
             return w_grouped[grp]
 
         def turn_wk(gp, r):
-            bank = transposes(wk_raw[(gp, r)][:].bitcast(F32), psum_a, "acc")
+            on_scalar = gp == 1 or r >= 2
+            bank = transposes(
+                wk_raw[(gp, r)][:].bitcast(F32), psum_s if on_scalar else psum_v, "bank_s" if on_scalar else "bank_v"
+            )
             words = (
                 grouped(0)[:]
                 .rearrange("p g n t -> p (g n t)")
@@ -221,7 +224,7 @@ def tile_stickyllamaattention_pa_kernel(tc, hidden_states, wq_bytes, wq_scale, w
                 .rearrange("p (g n u) -> p g n u", g=PASSES, n=N)
             )
             target = words[:, 2 * gp : 2 * gp + 2, P * r : P * (r + 1), :]
-            if gp == 1 and r > 0 or gp == 0 and r % 2 == 1:
+            if on_scalar:
                 nc.scalar.copy(out=target, in_=bank[:].rearrange("p u g n -> p g n u"))
             else:
                 nc.vector.tensor_copy(out=target, in_=bank[:].rearrange("p u g n -> p g n u"))
@@ -296,7 +299,8 @@ def tile_stickyllamaattention_pa_kernel(tc, hidden_states, wq_bytes, wq_scale, w
         accs = {}
 
         def project(step):
-            grp, pair = divmod(step, GROUP_STEPS)
+            pos, pair = divmod(step, GROUP_STEPS)
+            grp = ORDER[pos]
             for n in range(2):
                 acc = psum_a.tile([P, N], F32, name="acc")
                 accs[(step, n)] = acc
@@ -325,7 +329,7 @@ def tile_stickyllamaattention_pa_kernel(tc, hidden_states, wq_bytes, wq_scale, w
 
         def rope_products(step):
             products[step] = ropep.tile([P, GROUP_HEADS, 2, 2, 2, HALF], F32, name="products")
-            shared = step % GROUP_STEPS == 0 and step < STEPS - GROUP_STEPS
+            shared = step % GROUP_STEPS == GROUP_STEPS - 1 and step < STEPS - 2 * GROUP_STEPS
             if shared:
                 staged = stagep.tile([P, N], F32, name="staged")
                 nc.scalar.copy(out=staged[:], in_=accs[(step, 1)][:])
@@ -335,7 +339,8 @@ def tile_stickyllamaattention_pa_kernel(tc, hidden_states, wq_bytes, wq_scale, w
                 multiply(nc.vector, accs[(step, 1)], step, 1)
 
         def rope_sum(step):
-            grp, pair = divmod(step, GROUP_STEPS)
+            pos, pair = divmod(step, GROUP_STEPS)
+            grp = ORDER[pos]
             view = k_view if grp == 0 else q_view[:, GROUP_HEADS * (grp - 1) : GROUP_HEADS * grp, :, :]
             if step < STEPS - 1:
                 result = resultp.tile([P, GROUP_HEADS, 2, D], F32, name="result")
@@ -361,100 +366,97 @@ def tile_stickyllamaattention_pa_kernel(tc, hidden_states, wq_bytes, wq_scale, w
         first, last = (0, 1), (2, 3)
         every = first + last
 
+        turn_hidden(0)
+        widen(1, 0, every)
         for r in every:
             turn_wk(0, r)
-        for i in range(3):
-            turn_hidden(i)
-        widen(1, 0, first)
-        for r in every:
-            turn_wk(1, r)
-        quantize_hidden(0)
-        quantize_weights(0, 0)
         fill_table()
-        widen(1, 0, last)
-        turn_units(1, 0, first)
-        quantize_weights(0, 1)
-        turn_hidden(3)
-        scale_units(1, 0, first)
-        project(0)
-        turn_units(1, 0, last)
-        turn_hidden(4)
-
-        turn_hidden(5)
-        quantize_hidden(1)
-        scale_units(1, 0, last)
-        project(1)
-        quantize_weights(1, 0)
         widen(1, 1, first)
-        rope_products(0)
-        turn_units(1, 1, first)
+        turn_units(1, 0, first)
+        scale_units(1, 0, first)
+        turn_units(1, 0, last)
         widen(1, 1, last)
-        turn_hidden(6)
-        rope_sum(0)
-
-        rope_products(1)
-        quantize_hidden(2)
-        scale_units(1, 1, first)
-        turn_hidden(7)
-        widen(2, 0, every)
-        project(2)
-        rope_sum(1)
-        turn_units(1, 1, last)
-        turn_pass(2, 0)
+        turn_hidden(1)
+        turn_hidden(2)
+        scale_units(1, 0, last)
+        turn_units(1, 1, first)
         load_wq(3, 0)
         load_wq(3, 1)
-
-        quantize_hidden(3)
-        widen(2, 1, every)
-        scale_pass(2, 0)
-        project(3)
-        rope_products(2)
+        quantize_weights(1, 0)
+        turn_hidden(3)
+        scale_units(1, 1, first)
+        for r in first:
+            turn_wk(1, r)
+        quantize_hidden(0)
+        for r in last:
+            turn_wk(1, r)
+        turn_units(1, 1, last)
+        quantize_hidden(1)
+        turn_hidden(4)
         scale_units(1, 1, last)
-        rope_sum(2)
+        turn_hidden(5)
+        quantize_weights(0, 1)
+        turn_hidden(6)
+        quantize_weights(1, 1)
+        turn_hidden(7)
+        project(0)
+        quantize_hidden(2)
 
-        for step in range(3, STEPS):
-            phase = step % GROUP_STEPS
-            near = step // GROUP_STEPS + 1
-            far = near + 1
+        rope_products(0)
+        widen(2, 0, every)
+        widen(2, 1, every)
+        rope_sum(0)
+        quantize_hidden(3)
+        project(1)
+        turn_pass(2, 0)
+
+        rope_products(1)
+        rope_sum(1)
+        project(2)
+        quantize_weights(0, 0)
+        scale_pass(2, 0)
+
+        rope_products(2)
+        turn_pass(2, 1)
+        rope_sum(2)
+        project(3)
+
+        rope_products(3)
+        turn_units(2, 1, first)
+        rope_sum(3)
+        project(4)
+
+        for step in range(GROUP_STEPS, STEPS):
+            pos, phase = divmod(step, GROUP_STEPS)
+            near = pos + 1
+            far = pos + 2
             if near < GROUPS:
                 if phase == 0:
-                    scale_units(near, 1, first)
+                    scale_units(ORDER[near], 1, first)
+                    turn_units(ORDER[near], 1, last)
+                    scale_pass(ORDER[near], 1)
+                    interleave_pass(ORDER[near], 0)
                 if phase == 1:
-                    scale_units(near, 1, last)
-            if far < GROUPS:
-                if phase == 1:
-                    widen(far, 0, every)
+                    scale_units(ORDER[near], 1, last)
+                    interleave_pass(ORDER[near], 1)
                 if phase == 2:
-                    widen(far, 1, every)
+                    quantize_weights(ORDER[near], 0)
                 if phase == 3:
-                    interleave_pass(far, 0)
+                    quantize_weights(ORDER[near], 1)
+            if far < GROUPS:
                 if phase == 2:
-                    scale_pass(far, 0)
-            if near < GROUPS:
-                if phase == 0:
-                    scale_pass(near, 1)
-                if phase == 1:
-                    interleave_pass(near, 1)
-                if phase == 0:
-                    turn_units(near, 1, last)
-            if far < GROUPS and phase == 3:
-                turn_units(far, 1, first)
+                    turn_pass(ORDER[far], 0)
+                if phase == 3:
+                    turn_units(ORDER[far], 1, first)
+                    scale_pass(ORDER[far], 0)
+                    turn_pass(ORDER[far], 1)
             rope_products(step)
-            if phase == 3 and near == 1:
-                quantize_weights(1, 1)
-            if near < GROUPS:
-                if phase == 1:
-                    quantize_weights(near, 0)
-                if phase == 2:
-                    quantize_weights(near, 1)
-            rope_sum(step)
-            if far < GROUPS:
-                if phase == 1:
-                    turn_pass(far, 0)
-                if phase == 3:
-                    turn_pass(far, 1)
-            if step == 4:
-                load_wq(4, 0)
-                load_wq(4, 1)
             if step + 1 < STEPS:
                 project(step + 1)
+            rope_sum(step)
+            if far < GROUPS and phase == 1:
+                widen(ORDER[far], 0, every)
+                widen(ORDER[far], 1, every)
+            if step == GROUP_STEPS + 1:
+                load_wq(4, 0)
+                load_wq(4, 1)

@@ -97,12 +97,12 @@ def tile_stickyllamaattention_pa_kernel(tc, hidden_states, wq_bytes, wq_scale, w
             x_raw[i] = xpool.tile([P, H], BF16, name="x_raw")
             nc.sync.dma_start(out=x_raw[i][:], in_=hidden_tiles[i])
 
-        load_wq(1, 0)
         load_hidden(0)
+        load_wq(1, 0)
         load_wk(0)
         load_hidden(1)
-        load_hidden(2)
         load_wq(1, 1)
+        load_hidden(2)
         load_hidden(3)
         load_wk(1)
         for i in range(4, TOKEN_TILES):
@@ -329,7 +329,7 @@ def tile_stickyllamaattention_pa_kernel(tc, hidden_states, wq_bytes, wq_scale, w
 
         def rope_products(step):
             products[step] = ropep.tile([P, GROUP_HEADS, 2, 2, 2, HALF], F32, name="products")
-            shared = step % GROUP_STEPS == GROUP_STEPS - 1 and step < STEPS - 2 * GROUP_STEPS
+            shared = step % GROUP_STEPS == 0 and 0 < step < STEPS - GROUP_STEPS
             if shared:
                 staged = stagep.tile([P, N], F32, name="staged")
                 nc.scalar.copy(out=staged[:], in_=accs[(step, 1)][:])
@@ -367,64 +367,65 @@ def tile_stickyllamaattention_pa_kernel(tc, hidden_states, wq_bytes, wq_scale, w
         every = first + last
 
         turn_hidden(0)
-        widen(1, 0, every)
-        for r in every:
+        for r in first:
             turn_wk(0, r)
-        fill_table()
-        widen(1, 1, first)
+        widen(1, 0, every)
         turn_units(1, 0, first)
+        fill_table()
         scale_units(1, 0, first)
+        for r in last:
+            turn_wk(0, r)
+        widen(1, 1, every)
         turn_units(1, 0, last)
-        widen(1, 1, last)
         turn_hidden(1)
-        turn_hidden(2)
         scale_units(1, 0, last)
         turn_units(1, 1, first)
-        load_wq(3, 0)
-        load_wq(3, 1)
-        quantize_weights(1, 0)
+        turn_hidden(2)
         turn_hidden(3)
         scale_units(1, 1, first)
         for r in first:
             turn_wk(1, r)
+        quantize_weights(1, 0)
+        turn_units(1, 1, last)
+        load_wq(3, 0)
+        load_wq(3, 1)
         quantize_hidden(0)
         for r in last:
             turn_wk(1, r)
-        turn_units(1, 1, last)
-        quantize_hidden(1)
         turn_hidden(4)
         scale_units(1, 1, last)
+        quantize_hidden(1)
         turn_hidden(5)
-        quantize_weights(0, 1)
         turn_hidden(6)
-        quantize_weights(1, 1)
+        quantize_weights(0, 1)
         turn_hidden(7)
+        quantize_weights(1, 1)
         project(0)
-        quantize_hidden(2)
-
-        rope_products(0)
         widen(2, 0, every)
         widen(2, 1, every)
-        rope_sum(0)
+        quantize_hidden(2)
         quantize_hidden(3)
-        project(1)
-        turn_pass(2, 0)
 
-        rope_products(1)
-        rope_sum(1)
-        project(2)
-        quantize_weights(0, 0)
+        rope_products(0)
+        turn_pass(2, 0)
+        project(1)
         scale_pass(2, 0)
 
+        rope_products(1)
+        rope_sum(0)
+        quantize_weights(0, 0)
+        project(2)
+        turn_units(2, 1, first)
+        rope_sum(1)
+
         rope_products(2)
-        turn_pass(2, 1)
-        rope_sum(2)
         project(3)
+        turn_pass(2, 1)
 
         rope_products(3)
-        turn_units(2, 1, first)
-        rope_sum(3)
+        rope_sum(2)
         project(4)
+        rope_sum(3)
 
         for step in range(GROUP_STEPS, STEPS):
             pos, phase = divmod(step, GROUP_STEPS)
@@ -434,8 +435,8 @@ def tile_stickyllamaattention_pa_kernel(tc, hidden_states, wq_bytes, wq_scale, w
                 if phase == 0:
                     scale_units(ORDER[near], 1, first)
                     turn_units(ORDER[near], 1, last)
-                    scale_pass(ORDER[near], 1)
                     interleave_pass(ORDER[near], 0)
+                    scale_pass(ORDER[near], 1)
                 if phase == 1:
                     scale_units(ORDER[near], 1, last)
                     interleave_pass(ORDER[near], 1)
@@ -451,12 +452,12 @@ def tile_stickyllamaattention_pa_kernel(tc, hidden_states, wq_bytes, wq_scale, w
                     scale_pass(ORDER[far], 0)
                     turn_pass(ORDER[far], 1)
             rope_products(step)
-            if step + 1 < STEPS:
-                project(step + 1)
             rope_sum(step)
             if far < GROUPS and phase == 1:
                 widen(ORDER[far], 0, every)
                 widen(ORDER[far], 1, every)
+            if step + 1 < STEPS:
+                project(step + 1)
             if step == GROUP_STEPS + 1:
                 load_wq(4, 0)
                 load_wq(4, 1)

@@ -213,7 +213,7 @@ def tile_stickyllamaattention_pa_kernel(tc, hidden_states, wq_bytes, wq_scale, w
             return w_grouped[grp]
 
         def turn_wk(gp, r):
-            on_scalar = gp == 1 or r >= 2
+            on_scalar = gp == 1 or r > 0
             bank = transposes(
                 wk_raw[(gp, r)][:].bitcast(F32), psum_s if on_scalar else psum_v, "bank_s" if on_scalar else "bank_v"
             )
@@ -342,7 +342,7 @@ def tile_stickyllamaattention_pa_kernel(tc, hidden_states, wq_bytes, wq_scale, w
             pos, pair = divmod(step, GROUP_STEPS)
             grp = ORDER[pos]
             view = k_view if grp == 0 else q_view[:, GROUP_HEADS * (grp - 1) : GROUP_HEADS * grp, :, :]
-            if step < STEPS - 1:
+            if step < STEPS - 2:
                 result = resultp.tile([P, GROUP_HEADS, 2, D], F32, name="result")
                 nc.gpsimd.tensor_tensor(
                     out=result[:].rearrange("p h i (o j) -> p (h i o) j", o=2),
@@ -352,110 +352,109 @@ def tile_stickyllamaattention_pa_kernel(tc, hidden_states, wq_bytes, wq_scale, w
                 )
                 nc.sync.dma_start(out=view[:, :, 2 * pair : 2 * pair + 2, :], in_=result[:])
                 return
-            for n, engine in enumerate((nc.vector, nc.vector)):
-                result = widep.tile([P, GROUP_HEADS, D], F32, name="wide")
+            per = GROUP_HEADS // 2
+            for part in range(2):
+                heads = slice(per * part, per * (part + 1))
+                result = widep.tile([P, per, 2, D], F32, name="wide")
+                engine = nc.vector if step == STEPS - 1 else nc.gpsimd
                 engine.tensor_tensor(
-                    out=result[:].rearrange("p h (o j) -> p h o j", o=2),
-                    in0=products[step][:, :, n, :, 0, :],
-                    in1=products[step][:, :, n, :, 1, :],
+                    out=result[:].rearrange("p h i (o j) -> p (h i o) j", o=2),
+                    in0=products[step][:, heads, :, :, 0, :].rearrange("p h i o j -> p (h i o) j"),
+                    in1=products[step][:, heads, :, :, 1, :].rearrange("p h i o j -> p (h i o) j"),
                     op=ALU.add,
                 )
-                nc.sync.dma_start(out=view[:, :, 2 * pair + n, :], in_=result[:])
+                nc.sync.dma_start(out=view[:, heads, 2 * pair : 2 * pair + 2, :], in_=result[:])
 
         ctx.enter_context(tc.manual_schedule())
         first, last = (0, 1), (2, 3)
         every = first + last
 
         turn_hidden(0)
+        widen(1, 0, every)
+        fill_table()
         for r in first:
             turn_wk(0, r)
-        widen(1, 0, every)
         turn_units(1, 0, first)
-        fill_table()
         scale_units(1, 0, first)
         for r in last:
             turn_wk(0, r)
-        widen(1, 1, every)
         turn_units(1, 0, last)
-        turn_hidden(1)
+        widen(1, 1, first)
         scale_units(1, 0, last)
+        turn_hidden(1)
+        widen(1, 1, last)
+        quantize_hidden(0)
         turn_units(1, 1, first)
         turn_hidden(2)
         turn_hidden(3)
-        scale_units(1, 1, first)
         for r in first:
             turn_wk(1, r)
-        quantize_weights(1, 0)
+        scale_units(1, 1, first)
+        quantize_hidden(1)
         turn_units(1, 1, last)
-        load_wq(3, 0)
-        load_wq(3, 1)
-        quantize_hidden(0)
         for r in last:
             turn_wk(1, r)
-        turn_hidden(4)
         scale_units(1, 1, last)
-        quantize_hidden(1)
-        turn_hidden(5)
-        turn_hidden(6)
+        for i in (4, 5, 6):
+            turn_hidden(i)
+        quantize_weights(1, 0)
+        load_wq(3, 0)
+        load_wq(3, 1)
         quantize_weights(0, 1)
-        turn_hidden(7)
         quantize_weights(1, 1)
+        turn_hidden(7)
         project(0)
+        quantize_hidden(2)
         widen(2, 0, every)
         widen(2, 1, every)
-        quantize_hidden(2)
-        quantize_hidden(3)
+        turn_pass(2, 0)
+        quantize_weights(0, 0)
 
         rope_products(0)
-        turn_pass(2, 0)
+        quantize_hidden(3)
         project(1)
-        scale_pass(2, 0)
+        turn_units(2, 1, first)
 
         rope_products(1)
-        rope_sum(0)
-        quantize_weights(0, 0)
         project(2)
-        turn_units(2, 1, first)
-        rope_sum(1)
+        rope_sum(0)
 
         rope_products(2)
         project(3)
-        turn_pass(2, 1)
+        rope_sum(1)
 
         rope_products(3)
         rope_sum(2)
-        project(4)
+        scale_pass(2, 0)
+        turn_pass(2, 1)
         rope_sum(3)
+        project(4)
 
         for step in range(GROUP_STEPS, STEPS):
             pos, phase = divmod(step, GROUP_STEPS)
             near = pos + 1
             far = pos + 2
-            if near < GROUPS:
-                if phase == 0:
-                    scale_units(ORDER[near], 1, first)
-                    turn_units(ORDER[near], 1, last)
-                    interleave_pass(ORDER[near], 0)
-                    scale_pass(ORDER[near], 1)
-                if phase == 1:
-                    scale_units(ORDER[near], 1, last)
-                    interleave_pass(ORDER[near], 1)
-                if phase == 2:
-                    quantize_weights(ORDER[near], 0)
-                if phase == 3:
-                    quantize_weights(ORDER[near], 1)
-            if far < GROUPS:
-                if phase == 2:
-                    turn_pass(ORDER[far], 0)
-                if phase == 3:
-                    turn_units(ORDER[far], 1, first)
-                    scale_pass(ORDER[far], 0)
-                    turn_pass(ORDER[far], 1)
-            rope_products(step)
-            rope_sum(step)
+            if near < GROUPS and phase < 2:
+                interleave_pass(ORDER[near], phase)
+            if near < GROUPS and phase == 0:
+                scale_pass(ORDER[near], 1)
+            if far < GROUPS and phase == 3:
+                scale_pass(ORDER[far], 0)
+            if near < GROUPS and phase >= 2:
+                quantize_weights(ORDER[near], phase - 2)
+            if near < GROUPS and phase < 2:
+                scale_units(ORDER[near], 1, (first, last)[phase])
             if far < GROUPS and phase == 1:
                 widen(ORDER[far], 0, every)
                 widen(ORDER[far], 1, every)
+            rope_products(step)
+            rope_sum(step)
+            if far < GROUPS and phase >= 2:
+                turn_pass(ORDER[far], phase - 2)
+            if near < GROUPS and phase == 0:
+                turn_units(ORDER[near], 1, last)
+            if far < GROUPS and phase == 3:
+                turn_units(ORDER[far], 1, first)
             if step + 1 < STEPS:
                 project(step + 1)
             if step == GROUP_STEPS + 1:

@@ -262,6 +262,25 @@ def tile_stickyllamaattention_pa_kernel(tc, hidden_states, wq_bytes, wq_scale, w
                     op=ALU.mult,
                 )
 
+        def turn_last(grp, rows):
+            bank = psum_v.tile([P, 2, 2, P], F32, name="bank_v")
+            unit_banks[(grp, "last", rows)] = bank
+            for rr in range(2):
+                words = wides[(grp, 1, rows[rr])][:].bitcast(F32)
+                for u in range(2):
+                    nc.tensor.transpose(bank[:, u, rr, :], words[:, 256 + u : 512 : 2], ident[:])
+
+        def scale_last(grp, rows):
+            nc.vector.tensor_tensor(
+                out=grouped(grp)[:, PASSES - 1, P * rows[0] : P * (rows[1] + 1), :],
+                in0=unit_banks[(grp, "last", rows)][:]
+                .rearrange("p u r n -> p u (r n)")
+                .bitcast(BF16)
+                .rearrange("p u (m e) -> p m u e", e=2),
+                in1=scale4[:, PASSES - 1, :].unsqueeze(1).to_broadcast([P, 2 * P, 4]),
+                op=ALU.mult,
+            )
+
         pass_banks = {}
         planes = {}
 
@@ -329,7 +348,7 @@ def tile_stickyllamaattention_pa_kernel(tc, hidden_states, wq_bytes, wq_scale, w
 
         def rope_products(step):
             products[step] = ropep.tile([P, GROUP_HEADS, 2, 2, 2, HALF], F32, name="products")
-            shared = step % GROUP_STEPS == 0 and 0 < step < STEPS - GROUP_STEPS
+            shared = step % GROUP_STEPS == 0 and 0 < step < STEPS - 2 * GROUP_STEPS
             if shared:
                 staged = stagep.tile([P, N], F32, name="staged")
                 nc.scalar.copy(out=staged[:], in_=accs[(step, 1)][:])
@@ -378,83 +397,100 @@ def tile_stickyllamaattention_pa_kernel(tc, hidden_states, wq_bytes, wq_scale, w
         scale_units(1, 0, first)
         for r in last:
             turn_wk(0, r)
-        turn_units(1, 0, last)
         widen(1, 1, first)
+        turn_units(1, 0, last)
         scale_units(1, 0, last)
         turn_hidden(1)
-        widen(1, 1, last)
-        quantize_hidden(0)
         turn_units(1, 1, first)
+        scale_units(1, 1, first)
+        quantize_hidden(0)
+        widen(1, 1, last)
         turn_hidden(2)
-        turn_hidden(3)
         for r in first:
             turn_wk(1, r)
-        scale_units(1, 1, first)
-        quantize_hidden(1)
-        turn_units(1, 1, last)
-        for r in last:
-            turn_wk(1, r)
-        scale_units(1, 1, last)
-        for i in (4, 5, 6):
-            turn_hidden(i)
+        turn_hidden(3)
         quantize_weights(1, 0)
+        turn_units(1, 1, last)
+        turn_hidden(4)
+        scale_units(1, 1, last)
+        quantize_hidden(1)
         load_wq(3, 0)
         load_wq(3, 1)
-        quantize_weights(0, 1)
         quantize_weights(1, 1)
+        turn_hidden(5)
+        for r in last:
+            turn_wk(1, r)
+        quantize_hidden(2)
+        quantize_weights(0, 1)
+        turn_hidden(6)
         turn_hidden(7)
         project(0)
-        quantize_hidden(2)
         widen(2, 0, every)
         widen(2, 1, every)
         turn_pass(2, 0)
-        quantize_weights(0, 0)
 
         rope_products(0)
-        quantize_hidden(3)
+        rope_sum(0)
         project(1)
         turn_units(2, 1, first)
+        quantize_hidden(3)
 
         rope_products(1)
+        rope_sum(1)
         project(2)
-        rope_sum(0)
+        quantize_weights(0, 0)
 
         rope_products(2)
+        rope_sum(2)
         project(3)
-        rope_sum(1)
+        scale_pass(2, 0)
 
         rope_products(3)
-        rope_sum(2)
-        scale_pass(2, 0)
-        turn_pass(2, 1)
         rope_sum(3)
+        turn_pass(2, 1)
         project(4)
 
         for step in range(GROUP_STEPS, STEPS):
             pos, phase = divmod(step, GROUP_STEPS)
-            near = pos + 1
-            far = pos + 2
-            if near < GROUPS and phase < 2:
-                interleave_pass(ORDER[near], phase)
-            if near < GROUPS and phase == 0:
-                scale_pass(ORDER[near], 1)
-            if far < GROUPS and phase == 3:
-                scale_pass(ORDER[far], 0)
-            if near < GROUPS and phase >= 2:
-                quantize_weights(ORDER[near], phase - 2)
-            if near < GROUPS and phase < 2:
-                scale_units(ORDER[near], 1, (first, last)[phase])
-            if far < GROUPS and phase == 1:
-                widen(ORDER[far], 0, every)
-                widen(ORDER[far], 1, every)
+            near = ORDER[pos + 1] if pos + 1 < GROUPS else None
+            far = ORDER[pos + 2] if pos + 2 < GROUPS else None
+            final = ORDER[-1]
+            if near and phase < 2:
+                interleave_pass(near, phase)
+            if near == final and phase == 2:
+                interleave_pass(near, 2)
+            if near and phase >= 2:
+                quantize_weights(near, phase - 2)
+            if near and near != final and phase < 2:
+                scale_units(near, 1, (first, last)[phase])
+            if near == final and phase == 1:
+                scale_last(near, last)
+            if far == final and phase == 3:
+                scale_last(far, first)
+            if far and phase == 1:
+                widen(far, 0, every)
+                widen(far, 1, every)
+            if near and phase == 0:
+                scale_pass(near, 1)
+            if near == final and phase == 1:
+                scale_pass(near, 2)
+            if far and phase == 3:
+                scale_pass(far, 0)
+            if near and phase == 0:
+                if near == final:
+                    turn_last(near, last)
+                else:
+                    turn_units(near, 1, last)
+            if far == final and phase == 2:
+                turn_last(far, first)
+            if far and far != final and phase == 3:
+                turn_units(far, 1, first)
             rope_products(step)
             rope_sum(step)
-            if far < GROUPS and phase >= 2:
-                turn_pass(ORDER[far], phase - 2)
-            if near < GROUPS and phase == 0:
-                turn_units(ORDER[near], 1, last)
-            if far < GROUPS and phase == 3:
-                turn_units(ORDER[far], 1, first)
+            if near == final and phase == 0:
+                turn_pass(near, 2)
+            if far and phase >= 2:
+                turn_pass(far, phase - 2)
             if step + 1 < STEPS:
                 project(step + 1)
             if step == GROUP_STEPS + 1:

from contextlib import ExitStack

import concourse.mybir as mybir
from concourse.masks import make_identity

S, H, D = 1024, 2048, 128
Q_HEADS, KV_HEADS = 16, 4
ROPE_BASE, ROPE_FACTOR = 5.0e5, 8.0
LOW_FREQ, HIGH_FREQ, ORIG_MAX_POS = 1.0, 4.0, 8192

FLOPS = 2 * S * H * (Q_HEADS + KV_HEADS) * D

F32 = mybir.dt.float32
BF16 = mybir.dt.bfloat16
I32 = mybir.dt.int32
U32 = mybir.dt.uint32
U8 = mybir.dt.uint8
FP8 = mybir.dt.float8_e4m3fn
FP8X4 = mybir.dt.float8_e4m3fn_x4
ALU = mybir.AluOpType
ACT = mybir.ActivationFunctionType

P = 128
PASSES = H // (4 * P)
TOKEN_TILES = S // P
HALF = D // 2
GROUP_HEADS = 4
GROUPS = (Q_HEADS + KV_HEADS) // GROUP_HEADS
ORDER = (1, 0, 2, 3, 4)
N = GROUP_HEADS * D
GROUP_STEPS = TOKEN_TILES // 2
STEPS = GROUPS * GROUP_STEPS

PI = 3.141592653589793
TWO_PI = 2.0 * PI
TWO_PI_HIGH = 6.28125
TWO_PI_LOW = TWO_PI - TWO_PI_HIGH


def llama3_smooth(j):
    wavelen = TWO_PI * ROPE_BASE ** (2.0 * j / D)
    return min(max((ORIG_MAX_POS / wavelen - LOW_FREQ) / (HIGH_FREQ - LOW_FREQ), 0.0), 1.0)


def llama3_frequency(j):
    inv_freq = ROPE_BASE ** (-2.0 * j / D)
    smooth = llama3_smooth(j)
    return (1.0 - smooth) * inv_freq / ROPE_FACTOR + smooth * inv_freq


def tile_stickyllamaattention_pa_kernel(tc, hidden_states, wq_bytes, wq_scale, wk, out_0, out_1):
    nc = tc.nc

    hidden_tiles = hidden_states.rearrange("o (p i) k -> i p (o k)", i=TOKEN_TILES)
    wk_rows = wk.rearrange("(r p) k -> r p k", p=P)
    wq_halves = wq_bytes.rearrange("(c r p) (gp k) -> c gp p r k", r=GROUP_HEADS, p=P, gp=2)
    q_view = out_0.rearrange("o h (p i) d -> p (o h) i d", i=TOKEN_TILES)
    k_view = out_1.rearrange("o h (p i) d -> p (o h) i d", i=TOKEN_TILES)

    with ExitStack() as ctx:
        const = ctx.enter_context(tc.tile_pool(name="const", bufs=1))
        wkpool = ctx.enter_context(tc.tile_pool(name="wkpool", bufs=1))
        xpool = ctx.enter_context(tc.tile_pool(name="xpool", bufs=8))
        wqpool = ctx.enter_context(tc.tile_pool(name="wqpool", bufs=4))
        widep = ctx.enter_context(tc.tile_pool(name="widep", bufs=10))
        planesp = ctx.enter_context(tc.tile_pool(name="planesp", bufs=2))
        groupedp = ctx.enter_context(tc.tile_pool(name="groupedp", bufs=2))
        codes = ctx.enter_context(tc.tile_pool(name="codes", bufs=1))
        wcodes = ctx.enter_context(tc.tile_pool(name="wcodes", bufs=2))
        ropep = ctx.enter_context(tc.tile_pool(name="ropep", bufs=3))
        resultp = ctx.enter_context(tc.tile_pool(name="resultp", bufs=3))
        stagep = ctx.enter_context(tc.tile_pool(name="stagep", bufs=1))
        psum_v = ctx.enter_context(tc.psum_pool(name="psum_v", bufs=2))
        psum_s = ctx.enter_context(tc.psum_pool(name="psum_s", bufs=3))
        psum_a = ctx.enter_context(tc.psum_pool(name="psum_a", bufs=3))

        warm = const.tile([P, 2], F32, name="warm")
        nc.vector.memset(warm[:, 0:1], 0.0)
        nc.scalar.activation(out=warm[:, 1:2], in_=warm[:, 0:1], func=ACT.Sin)

        scale4 = const.tile([P, PASSES, 4], F32, name="scale4")
        nc.scalar.dma_start(out=scale4[:], in_=wq_scale.rearrange("o (g p t) -> p (o g) t", p=P, t=4))
        wk_raw = {}
        wq_raw = {}
        x_raw = {}

        def load_wk(gp):
            for r in range(GROUP_HEADS):
                wk_raw[(gp, r)] = wkpool.tile([P, H // 2], BF16, name="wk_raw%d_%d" % (gp, r))
                nc.sync.dma_start(out=wk_raw[(gp, r)][:], in_=wk_rows[r][:, 1024 * gp : 1024 * (gp + 1)])

        def load_wq(grp, gp):
            wq_raw[(grp, gp)] = wqpool.tile([P, GROUP_HEADS, H // 2], U8, name="wq_raw")
            nc.sync.dma_start(out=wq_raw[(grp, gp)][:], in_=wq_halves[grp - 1][gp])

        def load_hidden(i):
            x_raw[i] = xpool.tile([P, H], BF16, name="x_raw")
            nc.sync.dma_start(out=x_raw[i][:], in_=hidden_tiles[i])

        load_hidden(0)
        load_wq(1, 0)
        load_wk(0)
        load_hidden(1)
        load_wq(1, 1)
        load_hidden(2)
        load_hidden(3)
        load_wk(1)
        for i in range(4, TOKEN_TILES):
            load_hidden(i)
        load_wq(2, 0)
        load_wq(2, 1)

        ident = const.tile([P, P], F32, name="ident")
        make_identity(nc, ident[:])

        token_i = const.tile([P, TOKEN_TILES], I32, name="token_i")
        nc.gpsimd.iota(token_i[:], pattern=[[1, TOKEN_TILES]], base=0, channel_multiplier=TOKEN_TILES)
        token = const.tile([P, TOKEN_TILES], F32, name="token")
        nc.vector.tensor_copy(out=token[:], in_=token_i[:])

        freq = const.tile([P, HALF], F32, name="freq")
        nc.vector.memset(freq[:, 0:1], 1.0)
        for n in (1, 4, 16):
            for m in (n, 2 * n, 3 * n):
                factor = ROPE_BASE ** (-2.0 * m / D) / (ROPE_FACTOR if m >= HALF // 2 else 1.0)
                nc.vector.tensor_scalar(
                    out=freq[:, m : m + n], in0=freq[:, 0:n], scalar1=factor, scalar2=None, op0=ALU.mult
                )
        for j in range(HALF):
            if 0.0 < llama3_smooth(j) < 1.0:
                nc.vector.tensor_scalar(
                    out=freq[:, j : j + 1], in0=freq[:, 0:1], scalar1=llama3_frequency(j), scalar2=None, op0=ALU.mult
                )

        angle = const.tile([P, TOKEN_TILES, HALF], F32, name="angle")
        nc.vector.tensor_tensor(
            out=angle[:],
            in0=token[:].unsqueeze(2).to_broadcast([P, TOKEN_TILES, HALF]),
            in1=freq[:].unsqueeze(1).to_broadcast([P, TOKEN_TILES, HALF]),
            op=ALU.mult,
        )
        angle_flat = angle[:].rearrange("p i j -> p (i j)")
        turns = const.tile([P, TOKEN_TILES * HALF], I32, name="turns")
        nc.vector.tensor_scalar(out=turns[:], in0=angle_flat, scalar1=1.0 / TWO_PI, scalar2=None, op0=ALU.mult)
        part = const.tile([P, TOKEN_TILES * HALF], F32, name="part")
        nc.vector.scalar_tensor_tensor(
            out=part[:], in0=turns[:], scalar=-TWO_PI_HIGH, in1=angle_flat, op0=ALU.mult, op1=ALU.add
        )
        rest = const.tile([P, TOKEN_TILES, HALF], F32, name="rest")
        nc.vector.scalar_tensor_tensor(
            out=rest[:].rearrange("p i j -> p (i j)"), in0=turns[:], scalar=-TWO_PI_LOW, in1=part[:], op0=ALU.mult, op1=ALU.add
        )

        table = const.tile([P, TOKEN_TILES, 2, 2, HALF], F32, name="table")
        half_sin = const.tile([P, TOKEN_TILES, HALF], F32, name="half_sin")
        square = const.tile([P, TOKEN_TILES, HALF], F32, name="part")

        def fill_table():
            nc.scalar.activation(out=half_sin[:], in_=rest[:], func=ACT.Sin, scale=0.5)
            nc.scalar.activation(out=table[:, :, 1, 0, :], in_=rest[:], func=ACT.Sin)
            nc.gpsimd.tensor_tensor(out=square[:], in0=half_sin[:], in1=half_sin[:], op=ALU.mult)
            for half in range(2):
                nc.gpsimd.tensor_scalar(
                    out=table[:, :, half, half, :], in0=square[:], scalar1=-2.0, scalar2=1.0, op0=ALU.mult, op1=ALU.add
                )
            nc.gpsimd.tensor_scalar(
                out=table[:, :, 0, 1, :], in0=table[:, :, 1, 0, :], scalar1=-1.0, scalar2=0.0, op0=ALU.mult, op1=ALU.add
            )

        def transposes(words, pool, name):
            bank = pool.tile([P, 2, 2, P], F32, name=name)
            for gg in range(2):
                for u in range(2):
                    nc.tensor.transpose(bank[:, u, gg, :], words[:, 256 * gg + u : 256 * (gg + 1) : 2], ident[:])
            return bank

        x_codes = {}
        x_scales = {}
        x_grouped = {}

        def turn_hidden(i):
            pair = i // 2
            if i % 2 == 0:
                x_grouped[pair] = groupedp.tile([P, 2, PASSES, P, 4], BF16, name="x_grouped", align_bytes=64)
            words = (
                x_grouped[pair][:, i % 2, :, :, :]
                .rearrange("p g n t -> p (g n t)")
                .bitcast(F32)
                .rearrange("p (g n u) -> p g n u", g=PASSES, u=2)
            )
            for gp in range(2):
                bank = transposes(x_raw[i][:, 1024 * gp : 1024 * (gp + 1)].bitcast(F32), psum_s, "bank_s")
                nc.scalar.copy(out=words[:, 2 * gp : 2 * gp + 2, :, :], in_=bank[:].rearrange("p u g n -> p g n u"))

        def quantize_hidden(pair):
            x_codes[pair] = codes.tile([P, 2, PASSES * P], U32, name="x_codes%d" % pair, align_bytes=64)
            x_scales[pair] = codes.tile([P, 2, PASSES * P], U8, name="x_scales%d" % pair, align_bytes=64)
            nc.vector.quantize_mx(
                out=x_codes[pair][:].rearrange("p i c -> p (i c)").bitcast(FP8X4),
                scales=x_scales[pair][:].rearrange("p i c -> p (i c)"),
                in_=x_grouped[pair][:].rearrange("p i g n t -> p (i g n t)"),
            )

        w_grouped = {}
        w_codes = {}
        w_scales = {}

        def grouped(grp):
            if grp not in w_grouped:
                w_grouped[grp] = groupedp.tile([P, PASSES, N, 4], BF16, name="w_grouped", align_bytes=64)
                w_codes[grp] = wcodes.tile([P, PASSES, N], U32, name="w_codes", align_bytes=64)
                w_scales[grp] = wcodes.tile([P, PASSES, N], U8, name="w_scales", align_bytes=64)
            return w_grouped[grp]

        def turn_wk(gp, r):
            on_scalar = gp == 1 or r > 0
            bank = transposes(
                wk_raw[(gp, r)][:].bitcast(F32), psum_s if on_scalar else psum_v, "bank_s" if on_scalar else "bank_v"
            )
            words = (
                grouped(0)[:]
                .rearrange("p g n t -> p (g n t)")
                .bitcast(F32)
                .rearrange("p (g n u) -> p g n u", g=PASSES, n=N)
            )
            target = words[:, 2 * gp : 2 * gp + 2, P * r : P * (r + 1), :]
            if on_scalar:
                nc.scalar.copy(out=target, in_=bank[:].rearrange("p u g n -> p g n u"))
            else:
                nc.vector.tensor_copy(out=target, in_=bank[:].rearrange("p u g n -> p g n u"))

        def quantize_weights(grp, gp):
            passes = slice(2 * gp, 2 * gp + 2)
            nc.vector.quantize_mx(
                out=w_codes[grp][:, passes, :].rearrange("p g n -> p (g n)").bitcast(FP8X4),
                scales=w_scales[grp][:, passes, :].rearrange("p g n -> p (g n)"),
                in_=w_grouped[grp][:, passes, :, :].rearrange("p g n t -> p (g n t)"),
            )

        wides = {}

        def widen(grp, gp, rows):
            for r in rows:
                wides[(grp, gp, r)] = widep.tile([P, 1024], BF16, name="wide")
                nc.scalar.copy(out=wides[(grp, gp, r)][:], in_=wq_raw[(grp, gp)][:, r, :].bitcast(FP8))

        unit_banks = {}

        def turn_units(grp, gp, rows):
            for r in rows:
                unit_banks[(grp, gp, r)] = transposes(wides[(grp, gp, r)][:].bitcast(F32), psum_v, "bank_v")

        def scale_units(grp, gp, rows):
            for r in rows:
                nc.vector.tensor_tensor(
                    out=grouped(grp)[:, 2 * gp : 2 * gp + 2, P * r : P * (r + 1), :],
                    in0=unit_banks[(grp, gp, r)][:]
                    .rearrange("p u g n -> p u (g n)")
                    .bitcast(BF16)
                    .rearrange("p u (m e) -> p m u e", e=2),
                    in1=scale4[:, 2 * gp : 2 * gp + 2, :].unsqueeze(2).to_broadcast([P, 2, P, 4]),
                    op=ALU.mult,
                )

        def turn_last(grp, rows):
            bank = psum_v.tile([P, 2, 2, P], F32, name="bank_v")
            unit_banks[(grp, "last", rows)] = bank
            for rr in range(2):
                words = wides[(grp, 1, rows[rr])][:].bitcast(F32)
                for u in range(2):
                    nc.tensor.transpose(bank[:, u, rr, :], words[:, 256 + u : 512 : 2], ident[:])

        def scale_last(grp, rows):
            nc.vector.tensor_tensor(
                out=grouped(grp)[:, PASSES - 1, P * rows[0] : P * (rows[1] + 1), :],
                in0=unit_banks[(grp, "last", rows)][:]
                .rearrange("p u r n -> p u (r n)")
                .bitcast(BF16)
                .rearrange("p u (m e) -> p m u e", e=2),
                in1=scale4[:, PASSES - 1, :].unsqueeze(1).to_broadcast([P, 2 * P, 4]),
                op=ALU.mult,
            )

        pass_banks = {}
        planes = {}

        def turn_pass(grp, g):
            for u in range(2):
                pass_banks[(grp, g, u)] = psum_s.tile([P, GROUP_HEADS, P], F32, name="bank_s")
            for u in range(2):
                for r in range(GROUP_HEADS):
                    words = wides[(grp, g // 2, r)][:].bitcast(F32)
                    nc.tensor.transpose(
                        pass_banks[(grp, g, u)][:, r, :], words[:, 256 * (g % 2) + u : 256 * (g % 2 + 1) : 2], ident[:]
                    )

        def scale_pass(grp, g):
            planes[(grp, g)] = planesp.tile([P, 4, N], BF16, name="planes")
            for u in range(2):
                pairs = (
                    pass_banks[(grp, g, u)][:]
                    .rearrange("p r n -> p (r n)")
                    .bitcast(BF16)
                    .rearrange("p (m e) -> p m e", e=2)
                )
                for e in range(2):
                    t = 2 * u + e
                    nc.scalar.activation(
                        out=planes[(grp, g)][:, t, :], in_=pairs[:, :, e], func=ACT.Copy, scale=scale4[:, g, t : t + 1]
                    )

        def interleave_pass(grp, g):
            nc.scalar.copy(
                out=grouped(grp)[:, g, :, :].rearrange("p (c i) t -> p c t i", i=4),
                in_=planes[(grp, g)][:].rearrange("p t (c i) -> p c t i", i=4),
            )

        accs = {}

        def project(step):
            pos, pair = divmod(step, GROUP_STEPS)
            grp = ORDER[pos]
            for n in range(2):
                acc = psum_a.tile([P, N], F32, name="acc")
                accs[(step, n)] = acc
                for g in range(PASSES):
                    cols = slice(P * g, P * (g + 1))
                    nc.tensor.matmul_mx(
                        out=acc[:],
                        lhsT=x_codes[pair][:, n, cols].bitcast(FP8X4),
                        lhsT_scale=x_scales[pair][:, n, cols],
                        rhs=w_codes[grp][:, g, :].bitcast(FP8X4),
                        rhs_scale=w_scales[grp][:, g, :],
                        start=(g == 0),
                        stop=(g == PASSES - 1),
                    )

        products = {}

        def multiply(engine, source, step, n):
            i = 2 * (step % GROUP_STEPS) + n
            engine.tensor_tensor(
                out=products[step][:, :, n, :, :, :].rearrange("p h o s j -> p h o (s j)"),
                in0=source[:].rearrange("p (h d) -> p h d", h=GROUP_HEADS).unsqueeze(2).to_broadcast([P, GROUP_HEADS, 2, D]),
                in1=table[:, i, :, :, :].rearrange("p o s j -> p o (s j)").unsqueeze(1).to_broadcast([P, GROUP_HEADS, 2, D]),
                op=ALU.mult,
            )

        def rope_products(step):
            products[step] = ropep.tile([P, GROUP_HEADS, 2, 2, 2, HALF], F32, name="products")
            shared = step % GROUP_STEPS == 0 and 0 < step < STEPS - 2 * GROUP_STEPS
            if shared:
                staged = stagep.tile([P, N], F32, name="staged")
                nc.scalar.copy(out=staged[:], in_=accs[(step, 1)][:])
                multiply(nc.gpsimd, staged, step, 1)
            multiply(nc.vector, accs[(step, 0)], step, 0)
            if not shared:
                multiply(nc.vector, accs[(step, 1)], step, 1)

        def rope_sum(step):
            pos, pair = divmod(step, GROUP_STEPS)
            grp = ORDER[pos]
            view = k_view if grp == 0 else q_view[:, GROUP_HEADS * (grp - 1) : GROUP_HEADS * grp, :, :]
            if step < STEPS - 2:
                result = resultp.tile([P, GROUP_HEADS, 2, D], F32, name="result")
                nc.gpsimd.tensor_tensor(
                    out=result[:].rearrange("p h i (o j) -> p (h i o) j", o=2),
                    in0=products[step][:, :, :, :, 0, :].rearrange("p h i o j -> p (h i o) j"),
                    in1=products[step][:, :, :, :, 1, :].rearrange("p h i o j -> p (h i o) j"),
                    op=ALU.add,
                )
                nc.sync.dma_start(out=view[:, :, 2 * pair : 2 * pair + 2, :], in_=result[:])
                return
            per = GROUP_HEADS // 2
            for part in range(2):
                heads = slice(per * part, per * (part + 1))
                result = widep.tile([P, per, 2, D], F32, name="wide")
                engine = nc.vector if step == STEPS - 1 else nc.gpsimd
                engine.tensor_tensor(
                    out=result[:].rearrange("p h i (o j) -> p (h i o) j", o=2),
                    in0=products[step][:, heads, :, :, 0, :].rearrange("p h i o j -> p (h i o) j"),
                    in1=products[step][:, heads, :, :, 1, :].rearrange("p h i o j -> p (h i o) j"),
                    op=ALU.add,
                )
                nc.sync.dma_start(out=view[:, heads, 2 * pair : 2 * pair + 2, :], in_=result[:])

        ctx.enter_context(tc.manual_schedule())
        first, last = (0, 1), (2, 3)
        every = first + last

        turn_hidden(0)
        widen(1, 0, every)
        fill_table()
        for r in first:
            turn_wk(0, r)
        turn_units(1, 0, first)
        scale_units(1, 0, first)
        for r in last:
            turn_wk(0, r)
        widen(1, 1, first)
        turn_units(1, 0, last)
        scale_units(1, 0, last)
        turn_hidden(1)
        turn_units(1, 1, first)
        scale_units(1, 1, first)
        quantize_hidden(0)
        widen(1, 1, last)
        turn_hidden(2)
        for r in first:
            turn_wk(1, r)
        turn_hidden(3)
        quantize_weights(1, 0)
        turn_units(1, 1, last)
        turn_hidden(4)
        scale_units(1, 1, last)
        quantize_hidden(1)
        load_wq(3, 0)
        load_wq(3, 1)
        quantize_weights(1, 1)
        turn_hidden(5)
        for r in last:
            turn_wk(1, r)
        quantize_hidden(2)
        quantize_weights(0, 1)
        turn_hidden(6)
        turn_hidden(7)
        project(0)
        widen(2, 0, every)
        widen(2, 1, every)
        turn_pass(2, 0)

        rope_products(0)
        rope_sum(0)
        project(1)
        turn_units(2, 1, first)
        quantize_hidden(3)

        rope_products(1)
        rope_sum(1)
        project(2)
        quantize_weights(0, 0)

        rope_products(2)
        rope_sum(2)
        project(3)
        scale_pass(2, 0)

        rope_products(3)
        rope_sum(3)
        turn_pass(2, 1)
        project(4)

        for step in range(GROUP_STEPS, STEPS):
            pos, phase = divmod(step, GROUP_STEPS)
            near = ORDER[pos + 1] if pos + 1 < GROUPS else None
            far = ORDER[pos + 2] if pos + 2 < GROUPS else None
            final = ORDER[-1]
            if near and phase < 2:
                interleave_pass(near, phase)
            if near == final and phase == 2:
                interleave_pass(near, 2)
            if near and phase >= 2:
                quantize_weights(near, phase - 2)
            if near and near != final and phase < 2:
                scale_units(near, 1, (first, last)[phase])
            if near == final and phase == 1:
                scale_last(near, last)
            if far == final and phase == 3:
                scale_last(far, first)
            if far and phase == 1:
                widen(far, 0, every)
                widen(far, 1, every)
            if near and phase == 0:
                scale_pass(near, 1)
            if near == final and phase == 1:
                scale_pass(near, 2)
            if far and phase == 3:
                scale_pass(far, 0)
            if near and phase == 0:
                if near == final:
                    turn_last(near, last)
                else:
                    turn_units(near, 1, last)
            if far == final and phase == 2:
                turn_last(far, first)
            if far and far != final and phase == 3:
                turn_units(far, 1, first)
            rope_products(step)
            rope_sum(step)
            if near == final and phase == 0:
                turn_pass(near, 2)
            if far and phase >= 2:
                turn_pass(far, phase - 2)
            if step + 1 < STEPS:
                project(step + 1)
            if step == GROUP_STEPS + 1:
                load_wq(4, 0)
                load_wq(4, 1)
